import numpy as np
import ml_dtypes


def mxq(x, axis, fmt="e4m3"):
    dtype, down = {"e4m3": (ml_dtypes.float8_e4m3fn, 7), "e5m2": (ml_dtypes.float8_e5m2, 14)}[fmt]
    v = np.moveaxis(np.asarray(x, np.float32).astype(ml_dtypes.bfloat16).astype(np.float64), axis, -1)
    blocks = v.reshape(v.shape[:-1] + (-1, 32))
    amax = np.abs(blocks).max(-1, keepdims=True)
    byte = np.maximum(np.where(amax > 0, np.frexp(amax)[1] - 1 + 127, 0) - down, 1)
    scale = np.exp2(byte - 127.0)
    codes = (blocks / scale).astype(np.float32).astype(dtype).astype(np.float64)
    return np.moveaxis((codes * scale).reshape(v.shape), -1, axis)


WIDE = False


def mx_kscale(k):
    if not WIDE:
        return np.ones(k)
    levels = np.array([10, -10, 5, -5, 0])
    a = np.random.permutation(np.resize(levels, k // 512 * 4)).reshape(k // 512, 4)
    idx = np.arange(k)
    return np.exp2(a[idx // 512, idx % 128 // 32])


BF16 = ml_dtypes.bfloat16


def bf(x):
    return np.asarray(x, np.float32).astype(BF16)


def f64(x):
    return np.asarray(x).astype(np.float64)


B, N, HD, ED, F = 1, 64, 384, 256, 512
TD = HD + HD
MD = TD + ED
EPS = 1e-5


def layer_norm(x, g, b):
    mu = x.mean(-1, keepdims=True)
    var = x.var(-1, keepdims=True)
    return (x - mu) * (1.0 / np.sqrt(var + EPS)) * g + b


def setup_inputs():
    t = mx_kscale(F)
    rx = mx_kscale(MD)[:HD]
    r = np.concatenate([rx, rx, np.ones(ED)])
    return {"hid": bf(np.maximum(np.random.standard_normal((B, N, N, F)), 0.0) * t),
            "x_down": bf(np.random.standard_normal((B, N, HD)) * rx),
            "p_ln": bf(np.random.standard_normal((B, N, N, ED))),
            "W2": bf(np.random.standard_normal((F, MD)) / np.sqrt(F) / t[:, None] * r),
            "b2": bf(0.1 * np.random.standard_normal(MD) * r),
            "Wo": bf(np.random.standard_normal((MD, ED)) / np.sqrt(MD) / r[:, None]),
            "bo": bf(0.1 * np.random.standard_normal(ED)),
            "ln_out_g": bf(1.0 + 0.1 * np.random.standard_normal(ED)),
            "ln_out_b": bf(0.1 * np.random.standard_normal(ED))}


def reference(hid, x_down, p_ln, W2, b2, Wo, bo, ln_out_g, ln_out_b):
    xd, pl = f64(x_down), f64(p_ln)
    edge_bias = np.concatenate([np.broadcast_to(xd[:, :, None, :], (B, N, N, HD)),
                                np.broadcast_to(xd[:, None, :, :], (B, N, N, HD))], axis=-1)
    z_in = np.concatenate([edge_bias, pl], axis=-1)
    m = np.maximum((mxq(f64(hid), 3, "e4m3") @ mxq(f64(W2), 0, "e4m3")) + f64(b2), 0.0)
    z = (mxq(m + z_in, 3, "e4m3") @ mxq(f64(Wo), 0, "e4m3")) + f64(bo)
    return pl + layer_norm(z, f64(ln_out_g), f64(ln_out_b))

@@ -1,0 +1,451 @@
+from contextlib import ExitStack
+
+import concourse.mybir as mybir
+from concourse.masks import make_identity
+
+F32 = mybir.dt.float32
+BF16 = mybir.dt.bfloat16
+U32 = mybir.dt.uint32
+U8 = mybir.dt.uint8
+FP8X4 = mybir.dt.float8_e4m3fn_x4
+ALU = mybir.AluOpType
+ACT = mybir.ActivationFunctionType
+
+P = 128
+PACK = 4
+NODES = 64
+EDGES = NODES * NODES
+HID = 512
+NODE_F = 384
+EDGE_F = 256
+MID = 2 * NODE_F + EDGE_F
+EPS = 1e-5
+
+CHUNK = 512
+N_CHUNKS = EDGES // CHUNK
+TILES = CHUNK // P
+ROWS_I = CHUNK // NODES
+PLANES = MID // P
+HALF = CHUNK // 2
+
+FLOPS = 2 * EDGES * HID * MID + 2 * EDGES * MID * EDGE_F
+
+
+def tile_edgeupdaterwrapper_v01_pb_t_kernel(
+    tc, hid, x_down, p_ln, W2, b2, Wo, bo, ln_out_g, ln_out_b, out
+):
+    nc = tc.nc
+    hid_rows = hid.flatten_outer_dims()
+    p_rows = p_ln.flatten_outer_dims()
+    out_rows = out.flatten_outer_dims()
+    xd = x_down.flatten_outer_dims()
+
+    with ExitStack() as ctx:
+        keep = ctx.enter_context(tc.tile_pool(name="keep", bufs=1))
+        work = ctx.enter_context(tc.tile_pool(name="work", bufs=2))
+        psum = ctx.enter_context(tc.psum_pool(name="psum", bufs=1))
+
+        ident_f32 = keep.tile([P, P], F32)
+        make_identity(nc, ident_f32[:])
+        ident_bf = keep.tile([P, P], BF16)
+        make_identity(nc, ident_bf[:])
+        ctx.enter_context(tc.manual_schedule())
+        ones_bf = keep.tile([P, P], BF16)
+        nc.vector.memset(ones_bf[:], 1.0)
+        eps_col = keep.tile([P, 1], F32)
+        nc.vector.memset(eps_col[:], EPS)
+
+        xd2 = keep.tile([P, NODE_F], BF16)
+        nc.sync.dma_start(out=xd2[0:NODES, :], in_=xd)
+        nc.sync.dma_start(out=xd2[NODES:P, :], in_=xd)
+
+        b2_rows = keep.tile([P, P + HID], BF16)
+        nc.vector.memset(b2_rows[:], 0.0)
+        nc.sync.dma_start(out=b2_rows[0:4, 0:P], in_=b2[0:512].rearrange("(t c) -> t c", t=4))
+        b2_mixed = b2_rows[0:1, P : P + HID].rearrange("o (g k c) -> o g k c", g=2, k=2)
+        for k in range(2):
+            nc.sync.dma_start(
+                out=b2_mixed[:, :, k, :],
+                in_=b2[512 + 256 * k : 768 + 256 * k].rearrange("(o g c) -> o g c", o=1, g=2),
+            )
+
+        w2_raw = keep.tile([P, PACK, MID], BF16)
+        for u in range(2):
+            nc.sync.dma_start(
+                out=w2_raw[:, 2 * u : 2 * u + 2, :],
+                in_=W2[256 * u : 256 * u + 256, :].rearrange("(p h) f -> p h f", h=2),
+            )
+
+        hid_sb = keep.tile([P, EDGES // P, HID], BF16)
+        z_mixed = keep.tile([P, EDGES // P, HID], BF16)
+        z_cols = z_mixed[:].rearrange("p T (g k c) -> p T g k c", g=2, k=2)
+
+        def load_hid(c):
+            nc.sync.dma_start(
+                out=hid_sb[:, TILES * c : TILES * (c + 1), :],
+                in_=hid_rows[CHUNK * c : CHUNK * (c + 1), :].rearrange("(T p) k -> p T k", p=P),
+            )
+
+        def load_p_ln(c2):
+            for g in range(2):
+                nc.sync.dma_start(
+                    out=z_cols[:, 2 * TILES * c2 : 2 * TILES * (c2 + 1), g, 1, :],
+                    in_=p_rows[2 * CHUNK * c2 : 2 * CHUNK * (c2 + 1), P * g : P * (g + 1)].rearrange(
+                        "(T p) f -> p T f", p=P
+                    ),
+                )
+
+        load_hid(0)
+        load_p_ln(0)
+
+        wo_raw = keep.tile([P, 2, PACK, EDGE_F], BF16)
+        nc.sync.dma_start(out=wo_raw[:, 0, :, :], in_=Wo[0:512, :].rearrange("(t p) f -> p t f", p=P))
+        for k in range(2):
+            nc.sync.dma_start(
+                out=wo_raw[64 * k : 64 * k + 64, 1, :, :].rearrange("m (u h) f -> m u (h f)", h=2),
+                in_=Wo[512 + 256 * k : 768 + 256 * k, :].rearrange("(u m h) f -> m u (h f)", u=2, h=2),
+            )
+
+        vec_rows = keep.tile([P, 3 * EDGE_F], BF16)
+        nc.vector.memset(vec_rows[:], 0.0)
+        for n, vec in enumerate((bo, ln_out_g, ln_out_b)):
+            nc.gpsimd.dma_start(
+                out=vec_rows[0:1, EDGE_F * n : EDGE_F * (n + 1)],
+                in_=vec.rearrange("(o f) -> o f", o=1),
+            )
+
+        for c in range(1, N_CHUNKS):
+            load_hid(c)
+            if c % 2 == 0:
+                load_p_ln(c // 2)
+
+        for g in range(2):
+            nc.vector.tensor_copy(
+                out=z_cols[:, :, g, 0, :],
+                in_=xd2[:, P * (g + 1) : P * (g + 2)].unsqueeze(1).to_broadcast([P, EDGES // P, P]),
+            )
+
+        xt_ps = psum.tile([P, 4, P], BF16, tag="tr", bufs=2)
+        for t in range(3):
+            nc.tensor.transpose(xt_ps[:, t, :], xd2[:, P * t : P * (t + 1)], ident_bf[:])
+        nc.tensor.transpose(xt_ps[:, 3, :], b2_rows[:, 0:P], ident_bf[:])
+        xt = keep.tile([P, 4, P], F32)
+        nc.vector.tensor_copy(out=xt[:], in_=xt_ps[:])
+
+        neg_b = keep.tile([P, 4], F32)
+        nc.vector.tensor_scalar(
+            out=neg_b[:], in0=xt[:, 3, 0:4], scalar1=-1.0, scalar2=None, op0=ALU.mult
+        )
+        b_plus_z = keep.tile([P, 4, NODES], F32)
+        for t in range(4):
+            nc.vector.tensor_scalar(
+                out=b_plus_z[:, t, :],
+                in0=xt[:, t % 3, 0:NODES],
+                scalar1=xt[:, 3, t : t + 1],
+                scalar2=None,
+                op0=ALU.add,
+            )
+
+        b2m_ps = psum.tile([P, 2, P], F32, tag="tr", bufs=2)
+        for u in range(2):
+            nc.tensor.transpose(
+                b2m_ps[:, u, :],
+                b2_rows[:, P : P + HID].bitcast(F32)[:, P * u : P * (u + 1)],
+                ident_f32[:],
+            )
+        b2_hi = keep.tile([P, 4], F32)
+        nc.vector.tensor_copy(
+            out=b2_hi[:].rearrange("p (u h) -> p u h", h=2),
+            in_=b2m_ps[:].bitcast(BF16).rearrange("p u (n h) -> p u n h", h=2)[:, :, 0, :],
+        )
+
+        w2_grp = keep.tile([P, MID, PACK], BF16, align_bytes=64)
+        w2_codes = keep.tile([P, MID], U32, align_bytes=64)
+        w2_scales = keep.tile([P, MID], U8, align_bytes=64)
+        nc.vector.tensor_copy(
+            out=w2_grp[:, 0:512, :], in_=w2_raw[:, :, 0:512].rearrange("p t f -> p f t")
+        )
+        w2_hi = w2_raw[:, :, 512:1024].rearrange(
+            "p t (k u m h) -> p u h k m t", k=2, u=2, m=64, h=2
+        )
+        for u in range(2):
+            for h in range(2):
+                plane = 4 + 2 * u + h
+                nc.scalar.copy(
+                    out=w2_grp[:, P * plane : P * (plane + 1), :].rearrange(
+                        "p (k m) t -> p k m t", k=2
+                    ),
+                    in_=w2_hi[:, u, h],
+                )
+        for a in range(2):
+            nc.vector.quantize_mx(
+                out=w2_codes[:, 512 * a : 512 * (a + 1)].bitcast(FP8X4),
+                scales=w2_scales[:, 512 * a : 512 * (a + 1)],
+                in_=w2_grp[:, 512 * a : 512 * (a + 1), :].rearrange("p f t -> p (f t)"),
+            )
+
+        wo_grp = keep.tile([P, 2, EDGE_F, PACK], BF16, align_bytes=64)
+        wo_codes = keep.tile([P, 2 * EDGE_F], U32, align_bytes=64)
+        wo_scales = keep.tile([P, 2 * EDGE_F], U8, align_bytes=64)
+        bo_g = keep.tile([P, 2 * EDGE_F], F32)
+        bo_bc = bo_g[:, 0:EDGE_F]
+        g_bc = bo_g[:, EDGE_F : 2 * EDGE_F]
+
+        def prepare_stage2():
+            for a in range(2):
+                nc.vector.tensor_copy(
+                    out=wo_grp[:, a, :, :], in_=wo_raw[:, a, :, :].rearrange("p t f -> p f t")
+                )
+            nc.vector.quantize_mx(
+                out=wo_codes[:].bitcast(FP8X4),
+                scales=wo_scales[:],
+                in_=wo_grp[:].rearrange("p a f t -> p (a f t)"),
+            )
+            bc_ps = psum.tile([P, 2 * EDGE_F], F32, tag="h1", bufs=4)
+            nc.tensor.matmul(
+                bc_ps[:], lhsT=ones_bf[:], rhs=vec_rows[:, 0 : 2 * EDGE_F], start=True, stop=True
+            )
+            nc.vector.tensor_copy(out=bo_g[:], in_=bc_ps[:])
+
+        hid_grp_of = {}
+        hid_mx_of = {}
+        zt_of = {}
+        s_parts_of = {}
+        s_grp_of = {}
+        s_mx_of = {}
+        ln_of = {}
+
+        def transpose_words(rows, c, b):
+            words_t = psum.tile([P, 2, HALF], F32, tag="tr", bufs=2)
+            for u in range(2):
+                for l in range(2):
+                    nc.tensor.transpose(
+                        words_t[:, u, P * l : P * (l + 1)],
+                        rows[:, TILES * c + 2 * b + l, :].bitcast(F32)[:, P * u : P * (u + 1)],
+                        ident_f32[:],
+                    )
+            return words_t
+
+        def transposes(c):
+            hid_grp = work.tile([P, CHUNK * PACK], BF16, align_bytes=64)
+            hid_words = hid_grp[:].bitcast(F32).rearrange("p (e u) -> p e u", u=2)
+            for b in range(2):
+                hid_t = transpose_words(hid_sb, c, b)
+                nc.scalar.copy(
+                    out=hid_words[:, HALF * b : HALF * (b + 1), :],
+                    in_=hid_t[:].rearrange("p u e -> p e u"),
+                )
+            hid_grp_of[c] = hid_grp
+            zt_of[c] = [transpose_words(z_mixed, c, b) for b in range(2)]
+
+        def quantise_hid(c):
+            hid_codes = work.tile([P, CHUNK], U32, align_bytes=64)
+            hid_scales = work.tile([P, CHUNK], U8, align_bytes=64)
+            nc.vector.quantize_mx(
+                out=hid_codes[:].bitcast(FP8X4), scales=hid_scales[:], in_=hid_grp_of[c][:]
+            )
+            hid_mx_of[c] = (hid_codes, hid_scales)
+
+        def stage1(c):
+            hid_codes, hid_scales = hid_mx_of[c]
+            s_lo = work.tile([P, PACK, CHUNK], BF16)
+            r_hi = work.tile([P, PACK, CHUNK], F32)
+            s_parts_of[c] = (s_lo, r_hi)
+            for t in range(PACK):
+                for a in range(2):
+                    plane = PACK * a + t
+                    h1 = psum.tile([P, CHUNK], F32, tag="h1", bufs=4)
+                    nc.tensor.matmul_mx(
+                        out=h1[:],
+                        lhsT=w2_codes[:, P * plane : P * (plane + 1)].bitcast(FP8X4),
+                        lhsT_scale=w2_scales[:, P * plane : P * (plane + 1)],
+                        rhs=hid_codes[:].bitcast(FP8X4),
+                        rhs_scale=hid_scales[:],
+                        start=True,
+                        stop=True,
+                    )
+                    if a == 1:
+                        nc.scalar.activation(
+                            out=r_hi[:, t, :], in_=h1[:], func=ACT.Relu, bias=b2_hi[:, t : t + 1], scale=1.0
+                        )
+                        continue
+                    if t < 3:
+                        z_view = (
+                            b_plus_z[:, t, ROWS_I * c : ROWS_I * (c + 1)]
+                            .unsqueeze(2)
+                            .to_broadcast([P, ROWS_I, NODES])
+                        )
+                    else:
+                        z_view = b_plus_z[:, t, :].unsqueeze(1).to_broadcast([P, ROWS_I, NODES])
+                    nc.vector.scalar_tensor_tensor(
+                        out=s_lo[:, t, :].rearrange("p (i j) -> p i j", j=NODES),
+                        in0=h1[:].rearrange("p (i j) -> p i j", j=NODES),
+                        scalar=neg_b[:, t : t + 1],
+                        in1=z_view,
+                        op0=ALU.max,
+                        op1=ALU.add,
+                    )
+
+        def add_z(c):
+            s_lo, r_hi = s_parts_of[c]
+            s_grp = work.tile([P, 2, CHUNK * PACK], BF16, align_bytes=64)
+            s_grp_of[c] = s_grp
+            for b in range(2):
+                nc.vector.tensor_tensor(
+                    out=s_grp[:, 1, HALF * PACK * b : HALF * PACK * (b + 1)].rearrange(
+                        "p (e u h) -> p e u h", u=2, h=2
+                    ),
+                    in0=r_hi[:, :, HALF * b : HALF * (b + 1)].rearrange("p (u h) e -> p e u h", h=2),
+                    in1=zt_of[c][b][:].bitcast(BF16).rearrange("p u (e h) -> p e u h", h=2),
+                    op=ALU.add,
+                )
+
+        def regroup(c):
+            s_lo, r_hi = s_parts_of[c]
+            nc.scalar.copy(
+                out=s_grp_of[c][:, 0, :].rearrange("p (n i t) -> p n t i", i=4, t=PACK),
+                in_=s_lo[:].rearrange("p t (n i) -> p n t i", i=4),
+            )
+
+        def quantise_s(c):
+            s_codes = work.tile([P, 2, CHUNK], U32, align_bytes=64)
+            s_scales = work.tile([P, 2, CHUNK], U8, align_bytes=64)
+            for a in (1, 0):
+                nc.vector.quantize_mx(
+                    out=s_codes[:, a, :].bitcast(FP8X4),
+                    scales=s_scales[:, a, :],
+                    in_=s_grp_of[c][:, a, :],
+                )
+            s_mx_of[c] = (s_codes, s_scales)
+
+        def stage2(c):
+            s_codes, s_scales = s_mx_of[c]
+            zb = work.tile([P, TILES, EDGE_F], F32)
+            row_sum = work.tile([P, TILES], F32)
+            neg_mean = work.tile([P, TILES], F32)
+            for b in range(2):
+                z2 = psum.tile([P, 2, EDGE_F], F32, tag="ln", bufs=2)
+                for l in range(2):
+                    n = 2 * b + l
+                    for a in range(2):
+                        nc.tensor.matmul_mx(
+                            out=z2[:, l, :],
+                            lhsT=s_codes[:, a, P * n : P * (n + 1)].bitcast(FP8X4),
+                            lhsT_scale=s_scales[:, a, P * n : P * (n + 1)],
+                            rhs=wo_codes[:, EDGE_F * a : EDGE_F * (a + 1)].bitcast(FP8X4),
+                            rhs_scale=wo_scales[:, EDGE_F * a : EDGE_F * (a + 1)],
+                            start=(a == 0),
+                            stop=(a == 1),
+                        )
+                for l in range(2):
+                    n = 2 * b + l
+                    nc.vector.scalar_tensor_tensor(
+                        out=zb[:, n, :],
+                        in0=z2[:, l, :],
+                        scalar=1.0,
+                        in1=bo_bc,
+                        op0=ALU.mult,
+                        op1=ALU.add,
+                        accum_out=row_sum[:, n : n + 1],
+                    )
+            nc.vector.tensor_scalar(
+                out=neg_mean[:], in0=row_sum[:], scalar1=-1.0 / EDGE_F, scalar2=None, op0=ALU.mult
+            )
+            ln_of[c] = {"zb": zb, "neg_mean": neg_mean}
+
+        def variance(c):
+            zb = ln_of[c]["zb"]
+            neg_mean = ln_of[c]["neg_mean"]
+            squares = work.tile([P, TILES, EDGE_F], BF16)
+            sq_sum = work.tile([P, TILES], F32)
+            std = work.tile([P, TILES], F32)
+            for n in range(TILES):
+                nc.scalar.activation(
+                    out=squares[:, n, :],
+                    in_=zb[:, n, :],
+                    func=ACT.Square,
+                    bias=neg_mean[:, n : n + 1],
+                    scale=1.0,
+                    accum_out=sq_sum[:, n : n + 1],
+                )
+            nc.scalar.activation(
+                out=std[:], in_=sq_sum[:], func=ACT.Sqrt, bias=eps_col[:], scale=1.0 / EDGE_F
+            )
+            ln_of[c]["std"] = std
+
+        def residual(c):
+            q_banks = []
+            for b in range(2):
+                q_ps = psum.tile([P, 2, EDGE_F], F32, tag="ln", bufs=2)
+                for l in range(2):
+                    nc.tensor.matmul(
+                        q_ps[:, l, :].rearrange("p (g f) -> p g f", g=2),
+                        lhsT=ident_bf[:],
+                        rhs=z_cols[:, TILES * c + 2 * b + l, :, 1, :],
+                        start=True,
+                        stop=False,
+                    )
+                    nc.tensor.matmul(
+                        q_ps[:, l, :],
+                        lhsT=ones_bf[:],
+                        rhs=vec_rows[:, 2 * EDGE_F : 3 * EDGE_F],
+                        start=False,
+                        stop=True,
+                    )
+                q_banks.append(q_ps)
+            ln_of[c]["q"] = q_banks
+
+        def normalise(c):
+            zb = ln_of[c]["zb"]
+            neg_mean = ln_of[c]["neg_mean"]
+            rstd = work.tile([P, TILES], F32)
+            scaled = work.tile([P, TILES, EDGE_F], F32)
+            result = work.tile([P, TILES, EDGE_F], F32)
+            nc.vector.reciprocal(out=rstd[:], in_=ln_of[c]["std"][:])
+            for n in range(TILES):
+                nc.vector.scalar_tensor_tensor(
+                    out=scaled[:, n, :],
+                    in0=zb[:, n, :],
+                    scalar=neg_mean[:, n : n + 1],
+                    in1=g_bc,
+                    op0=ALU.add,
+                    op1=ALU.mult,
+                )
+                nc.vector.scalar_tensor_tensor(
+                    out=result[:, n, :],
+                    in0=scaled[:, n, :],
+                    scalar=rstd[:, n : n + 1],
+                    in1=ln_of[c]["q"][n // 2][:, n % 2, :],
+                    op0=ALU.mult,
+                    op1=ALU.add,
+                )
+            nc.sync.dma_start(
+                out=out_rows[CHUNK * c : CHUNK * (c + 1), :].rearrange("(T p) f -> p T f", p=P),
+                in_=result[:],
+            )
+
+        transposes(0)
+        quantise_hid(0)
+        stage1(0)
+        prepare_stage2()
+        add_z(0)
+        regroup(0)
+        quantise_s(0)
+        transposes(1)
+        quantise_hid(1)
+        for j in range(1, N_CHUNKS):
+            stage2(j - 1)
+            stage1(j)
+            variance(j - 1)
+            residual(j - 1)
+            add_z(j)
+            regroup(j)
+            normalise(j - 1)
+            quantise_s(j)
+            if j + 1 < N_CHUNKS:
+                transposes(j + 1)
+                quantise_hid(j + 1)
+        stage2(N_CHUNKS - 1)
+        variance(N_CHUNKS - 1)
+        residual(N_CHUNKS - 1)
+        normalise(N_CHUNKS - 1)

@@ -208,35 +208,36 @@ def tile_edgeupdaterwrapper_v01_pb_t_kernel(
             nc.vector.tensor_copy(out=bo_g[:], in_=bc_ps[:])
 
         hid_grp_of = {}
+        z_grp_of = {}
         hid_mx_of = {}
-        zt_of = {}
         s_parts_of = {}
         s_grp_of = {}
         s_mx_of = {}
         ln_of = {}
 
-        def transpose_words(rows, c, b):
-            words_t = psum.tile([P, 2, HALF], F32, tag="tr", bufs=2)
-            for u in range(2):
-                for l in range(2):
-                    nc.tensor.transpose(
-                        words_t[:, u, P * l : P * (l + 1)],
-                        rows[:, TILES * c + 2 * b + l, :].bitcast(F32)[:, P * u : P * (u + 1)],
-                        ident_f32[:],
-                    )
-            return words_t
+        def transpose_words(rows, c, grouped):
+            words = grouped[:].bitcast(F32).rearrange("p (e u) -> p e u", u=2)
+            for b in range(2):
+                words_t = psum.tile([P, 2, HALF], F32, tag="tr", bufs=2)
+                for u in range(2):
+                    for l in range(2):
+                        nc.tensor.transpose(
+                            words_t[:, u, P * l : P * (l + 1)],
+                            rows[:, TILES * c + 2 * b + l, :].bitcast(F32)[:, P * u : P * (u + 1)],
+                            ident_f32[:],
+                        )
+                nc.scalar.copy(
+                    out=words[:, HALF * b : HALF * (b + 1), :],
+                    in_=words_t[:].rearrange("p u e -> p e u"),
+                )
 
         def transposes(c):
-            hid_grp = work.tile([P, CHUNK * PACK], BF16, align_bytes=64)
-            hid_words = hid_grp[:].bitcast(F32).rearrange("p (e u) -> p e u", u=2)
-            for b in range(2):
-                hid_t = transpose_words(hid_sb, c, b)
-                nc.scalar.copy(
-                    out=hid_words[:, HALF * b : HALF * (b + 1), :],
-                    in_=hid_t[:].rearrange("p u e -> p e u"),
-                )
+            hid_grp = work.tile([P, CHUNK * PACK], BF16, align_bytes=64, bufs=2)
+            transpose_words(hid_sb, c, hid_grp)
             hid_grp_of[c] = hid_grp
-            zt_of[c] = [transpose_words(z_mixed, c, b) for b in range(2)]
+            z_grp = work.tile([P, CHUNK * PACK], BF16, bufs=4)
+            transpose_words(z_mixed, c, z_grp)
+            z_grp_of[c] = z_grp
 
         def quantise_hid(c):
             hid_codes = work.tile([P, CHUNK], U32, align_bytes=64)
@@ -252,7 +253,7 @@ def tile_edgeupdaterwrapper_v01_pb_t_kernel(
             r_hi = work.tile([P, PACK, CHUNK], F32)
             s_parts_of[c] = (s_lo, r_hi)
             for t in range(PACK):
-                for a in range(2):
+                for a in (1, 0):
                     plane = PACK * a + t
                     h1 = psum.tile([P, CHUNK], F32, tag="h1", bufs=4)
                     nc.tensor.matmul_mx(
@@ -286,26 +287,29 @@ def tile_edgeupdaterwrapper_v01_pb_t_kernel(
                         op1=ALU.add,
                     )
 
-        def add_z(c):
+        def group_s(c):
             s_lo, r_hi = s_parts_of[c]
-            s_grp = work.tile([P, 2, CHUNK * PACK], BF16, align_bytes=64)
+            s_grp = work.tile([P, 2, CHUNK, PACK], BF16, align_bytes=64)
             s_grp_of[c] = s_grp
+            z_words = z_grp_of[c][:].rearrange("p (e t) -> p e t", t=PACK)
             for b in range(2):
-                nc.vector.tensor_tensor(
-                    out=s_grp[:, 1, HALF * PACK * b : HALF * PACK * (b + 1)].rearrange(
-                        "p (e u h) -> p e u h", u=2, h=2
-                    ),
-                    in0=r_hi[:, :, HALF * b : HALF * (b + 1)].rearrange("p (u h) e -> p e u h", h=2),
-                    in1=zt_of[c][b][:].bitcast(BF16).rearrange("p u (e h) -> p e u h", h=2),
+                edges = slice(HALF * b, HALF * (b + 1))
+                nc.gpsimd.tensor_tensor(
+                    out=s_grp[:, 1, edges, :],
+                    in0=r_hi[:, :, edges].rearrange("p t e -> p e t"),
+                    in1=z_words[:, edges, :],
                     op=ALU.add,
                 )
-
-        def regroup(c):
-            s_lo, r_hi = s_parts_of[c]
-            nc.scalar.copy(
-                out=s_grp_of[c][:, 0, :].rearrange("p (n i t) -> p n t i", i=4, t=PACK),
-                in_=s_lo[:].rearrange("p t (n i) -> p n t i", i=4),
-            )
+            for b in range(2):
+                edges = slice(HALF * b, HALF * (b + 1))
+                nc.gpsimd.tensor_scalar(
+                    out=s_grp[:, 0, edges, :],
+                    in0=s_lo[:, :, edges].rearrange("p t e -> p e t"),
+                    scalar1=1.0,
+                    scalar2=0.0,
+                    op0=ALU.mult,
+                    op1=ALU.add,
+                )
 
         def quantise_s(c):
             s_codes = work.tile([P, 2, CHUNK], U32, align_bytes=64)
@@ -314,15 +318,15 @@ def tile_edgeupdaterwrapper_v01_pb_t_kernel(
                 nc.vector.quantize_mx(
                     out=s_codes[:, a, :].bitcast(FP8X4),
                     scales=s_scales[:, a, :],
-                    in_=s_grp_of[c][:, a, :],
+                    in_=s_grp_of[c][:, a, :, :].rearrange("p e t -> p (e t)"),
                 )
             s_mx_of[c] = (s_codes, s_scales)
 
         def stage2(c):
             s_codes, s_scales = s_mx_of[c]
-            zb = work.tile([P, TILES, EDGE_F], F32)
+            zb = work.tile([P, TILES, EDGE_F], F32, bufs=3)
             row_sum = work.tile([P, TILES], F32)
-            neg_mean = work.tile([P, TILES], F32)
+            neg_mean = work.tile([P, TILES], F32, bufs=4)
             for b in range(2):
                 z2 = psum.tile([P, 2, EDGE_F], F32, tag="ln", bufs=2)
                 for l in range(2):
@@ -358,7 +362,7 @@ def tile_edgeupdaterwrapper_v01_pb_t_kernel(
             neg_mean = ln_of[c]["neg_mean"]
             squares = work.tile([P, TILES, EDGE_F], BF16)
             sq_sum = work.tile([P, TILES], F32)
-            std = work.tile([P, TILES], F32)
+            std = work.tile([P, TILES], F32, bufs=3)
             for n in range(TILES):
                 nc.scalar.activation(
                     out=squares[:, n, :],
@@ -393,59 +397,68 @@ def tile_edgeupdaterwrapper_v01_pb_t_kernel(
                         stop=True,
                     )
                 q_banks.append(q_ps)
+            rstd = work.tile([P, TILES], F32)
+            nc.vector.reciprocal(out=rstd[:], in_=ln_of[c]["std"][:])
+            result = work.tile([P, TILES, EDGE_F], F32)
             ln_of[c]["q"] = q_banks
+            ln_of[c]["rstd"] = rstd
+            ln_of[c]["result"] = result
 
-        def normalise(c):
+        def normalise(c, b):
             zb = ln_of[c]["zb"]
             neg_mean = ln_of[c]["neg_mean"]
-            rstd = work.tile([P, TILES], F32)
-            scaled = work.tile([P, TILES, EDGE_F], F32)
-            result = work.tile([P, TILES, EDGE_F], F32)
-            nc.vector.reciprocal(out=rstd[:], in_=ln_of[c]["std"][:])
-            for n in range(TILES):
+            rstd = ln_of[c]["rstd"]
+            result = ln_of[c]["result"]
+            scaled = work.tile([P, 2, EDGE_F], F32)
+            for l in range(2):
+                n = 2 * b + l
                 nc.vector.scalar_tensor_tensor(
-                    out=scaled[:, n, :],
+                    out=scaled[:, l, :],
                     in0=zb[:, n, :],
                     scalar=neg_mean[:, n : n + 1],
                     in1=g_bc,
                     op0=ALU.add,
                     op1=ALU.mult,
                 )
+            for l in range(2):
+                n = 2 * b + l
                 nc.vector.scalar_tensor_tensor(
                     out=result[:, n, :],
-                    in0=scaled[:, n, :],
+                    in0=scaled[:, l, :],
                     scalar=rstd[:, n : n + 1],
-                    in1=ln_of[c]["q"][n // 2][:, n % 2, :],
+                    in1=ln_of[c]["q"][b][:, l, :],
                     op0=ALU.mult,
                     op1=ALU.add,
                 )
+
+        def store(c):
             nc.sync.dma_start(
                 out=out_rows[CHUNK * c : CHUNK * (c + 1), :].rearrange("(T p) f -> p T f", p=P),
-                in_=result[:],
+                in_=ln_of[c]["result"][:],
             )
 
-        transposes(0)
-        quantise_hid(0)
-        stage1(0)
-        prepare_stage2()
-        add_z(0)
-        regroup(0)
-        quantise_s(0)
-        transposes(1)
-        quantise_hid(1)
-        for j in range(1, N_CHUNKS):
-            stage2(j - 1)
-            stage1(j)
-            variance(j - 1)
-            residual(j - 1)
-            add_z(j)
-            regroup(j)
-            normalise(j - 1)
-            quantise_s(j)
-            if j + 1 < N_CHUNKS:
-                transposes(j + 1)
+        def live(c):
+            return 0 <= c < N_CHUNKS
+
+        for j in range(-2, N_CHUNKS + 3):
+            if live(j):
+                stage1(j)
+                group_s(j)
+            if j == 0:
+                prepare_stage2()
+            if live(j - 3):
+                residual(j - 3)
+                normalise(j - 3, 0)
+            if live(j - 1):
+                quantise_s(j - 1)
+            if live(j - 3):
+                normalise(j - 3, 1)
+                store(j - 3)
+            if live(j + 1):
                 quantise_hid(j + 1)
-        stage2(N_CHUNKS - 1)
-        variance(N_CHUNKS - 1)
-        residual(N_CHUNKS - 1)
-        normalise(N_CHUNKS - 1)
+            if live(j - 2):
+                variance(j - 2)
+            if live(j + 2):
+                transposes(j + 2)
+            if live(j - 1):
+                stage2(j - 1)

@@ -27,6 +27,7 @@ TILES = CHUNK // P
 ROWS_I = CHUNK // NODES
 PLANES = MID // P
 HALF = CHUNK // 2
+RUN = 4
 
 FLOPS = 2 * EDGES * HID * MID + 2 * EDGES * MID * EDGE_F
 
@@ -291,20 +292,20 @@ def tile_edgeupdaterwrapper_v01_pb_t_kernel(
             s_lo, r_hi = s_parts_of[c]
             s_grp = work.tile([P, 2, CHUNK, PACK], BF16, align_bytes=64)
             s_grp_of[c] = s_grp
-            z_words = z_grp_of[c][:].rearrange("p (e t) -> p e t", t=PACK)
+            z_runs = z_grp_of[c][:].rearrange("p (n i t) -> p n t i", i=RUN, t=PACK)
             for b in range(2):
-                edges = slice(HALF * b, HALF * (b + 1))
+                runs = slice(HALF // RUN * b, HALF // RUN * (b + 1))
                 nc.gpsimd.tensor_tensor(
-                    out=s_grp[:, 1, edges, :],
-                    in0=r_hi[:, :, edges].rearrange("p t e -> p e t"),
-                    in1=z_words[:, edges, :],
+                    out=s_grp[:, 1, :, :].rearrange("p (n i) t -> p n t i", i=RUN)[:, runs],
+                    in0=r_hi[:].rearrange("p t (n i) -> p n t i", i=RUN)[:, runs],
+                    in1=z_runs[:, runs],
                     op=ALU.add,
                 )
             for b in range(2):
-                edges = slice(HALF * b, HALF * (b + 1))
+                runs = slice(HALF // RUN * b, HALF // RUN * (b + 1))
                 nc.gpsimd.tensor_scalar(
-                    out=s_grp[:, 0, edges, :],
-                    in0=s_lo[:, :, edges].rearrange("p t e -> p e t"),
+                    out=s_grp[:, 0, :, :].rearrange("p (n i) t -> p n t i", i=RUN)[:, runs],
+                    in0=s_lo[:].rearrange("p t (n i) -> p n t i", i=RUN)[:, runs],
                     scalar1=1.0,
                     scalar2=0.0,
                     op0=ALU.mult,

@@ -253,6 +253,8 @@ def tile_edgeupdaterwrapper_v01_pb_t_kernel(
             s_lo = work.tile([P, PACK, CHUNK], BF16)
             r_hi = work.tile([P, PACK, CHUNK], F32)
             s_parts_of[c] = (s_lo, r_hi)
+            s_grp = work.tile([P, 2, CHUNK, PACK], BF16, align_bytes=64)
+            s_grp_of[c] = s_grp
             for t in range(PACK):
                 for a in (1, 0):
                     plane = PACK * a + t
@@ -288,34 +290,27 @@ def tile_edgeupdaterwrapper_v01_pb_t_kernel(
                         op1=ALU.add,
                     )
 
-        def group_s(c):
+        def add_z(engine, c, b):
             s_lo, r_hi = s_parts_of[c]
-            s_grp = work.tile([P, 2, CHUNK, PACK], BF16, align_bytes=64)
-            s_grp_of[c] = s_grp
-            z_runs = z_grp_of[c][:].rearrange("p (n i t) -> p n t i", i=RUN, t=PACK)
-            for b in range(2):
-                runs = slice(HALF // RUN * b, HALF // RUN * (b + 1))
-                nc.gpsimd.tensor_tensor(
-                    out=s_grp[:, 1, :, :].rearrange("p (n i) t -> p n t i", i=RUN)[:, runs],
-                    in0=r_hi[:].rearrange("p t (n i) -> p n t i", i=RUN)[:, runs],
-                    in1=z_runs[:, runs],
-                    op=ALU.add,
-                )
-            for b in range(2):
-                runs = slice(HALF // RUN * b, HALF // RUN * (b + 1))
-                nc.gpsimd.tensor_scalar(
-                    out=s_grp[:, 0, :, :].rearrange("p (n i) t -> p n t i", i=RUN)[:, runs],
-                    in0=s_lo[:].rearrange("p t (n i) -> p n t i", i=RUN)[:, runs],
-                    scalar1=1.0,
-                    scalar2=0.0,
-                    op0=ALU.mult,
-                    op1=ALU.add,
-                )
+            edges = slice(HALF * b, HALF * (b + 1))
+            engine.tensor_tensor(
+                out=s_grp_of[c][:, 1, edges, :],
+                in0=r_hi[:, :, edges].rearrange("p t e -> p e t"),
+                in1=z_grp_of[c][:].rearrange("p (e t) -> p e t", t=PACK)[:, edges, :],
+                op=ALU.add,
+            )
+
+        def regroup(c):
+            s_lo, r_hi = s_parts_of[c]
+            nc.scalar.copy(
+                out=s_grp_of[c][:, 0, :, :].rearrange("p (n i) t -> p n t i", i=RUN),
+                in_=s_lo[:].rearrange("p t (n i) -> p n t i", i=RUN),
+            )
 
         def quantise_s(c):
             s_codes = work.tile([P, 2, CHUNK], U32, align_bytes=64)
             s_scales = work.tile([P, 2, CHUNK], U8, align_bytes=64)
-            for a in (1, 0):
+            for a in range(2):
                 nc.vector.quantize_mx(
                     out=s_codes[:, a, :].bitcast(FP8X4),
                     scales=s_scales[:, a, :],
@@ -441,25 +436,27 @@ def tile_edgeupdaterwrapper_v01_pb_t_kernel(
         def live(c):
             return 0 <= c < N_CHUNKS
 
-        for j in range(-2, N_CHUNKS + 3):
+        for j in range(-1, N_CHUNKS + 3):
             if live(j):
                 stage1(j)
-                group_s(j)
+                add_z(nc.gpsimd, j, 1)
+            if live(j + 1):
+                transposes(j + 1)
+            if live(j):
+                regroup(j)
             if j == 0:
                 prepare_stage2()
+            if live(j - 1):
+                add_z(nc.vector, j - 1, 0)
+                quantise_s(j - 1)
+            if live(j + 1):
+                quantise_hid(j + 1)
             if live(j - 3):
                 residual(j - 3)
                 normalise(j - 3, 0)
-            if live(j - 1):
-                quantise_s(j - 1)
-            if live(j - 3):
                 normalise(j - 3, 1)
                 store(j - 3)
-            if live(j + 1):
-                quantise_hid(j + 1)
-            if live(j - 2):
-                variance(j - 2)
-            if live(j + 2):
-                transposes(j + 2)
             if live(j - 1):
                 stage2(j - 1)
+            if live(j - 2):
+                variance(j - 2)

@@ -253,10 +253,11 @@ def tile_edgeupdaterwrapper_v01_pb_t_kernel(
             s_lo = work.tile([P, PACK, CHUNK], BF16)
             r_hi = work.tile([P, PACK, CHUNK], F32)
             s_parts_of[c] = (s_lo, r_hi)
-            s_grp = work.tile([P, 2, CHUNK, PACK], BF16, align_bytes=64)
-            s_grp_of[c] = s_grp
-            for t in range(PACK):
-                for a in (1, 0):
+            s_grp_lo = work.tile([P, CHUNK, PACK], BF16, align_bytes=64)
+            s_grp_hi = work.tile([P, CHUNK, PACK], BF16, align_bytes=64, bufs=1)
+            s_grp_of[c] = (s_grp_lo, s_grp_hi)
+            for a in (1, 0):
+                for t in range(PACK):
                     plane = PACK * a + t
                     h1 = psum.tile([P, CHUNK], F32, tag="h1", bufs=4)
                     nc.tensor.matmul_mx(
@@ -294,7 +295,7 @@ def tile_edgeupdaterwrapper_v01_pb_t_kernel(
             s_lo, r_hi = s_parts_of[c]
             edges = slice(HALF * b, HALF * (b + 1))
             engine.tensor_tensor(
-                out=s_grp_of[c][:, 1, edges, :],
+                out=s_grp_of[c][1][:, edges, :],
                 in0=r_hi[:, :, edges].rearrange("p t e -> p e t"),
                 in1=z_grp_of[c][:].rearrange("p (e t) -> p e t", t=PACK)[:, edges, :],
                 op=ALU.add,
@@ -303,7 +304,7 @@ def tile_edgeupdaterwrapper_v01_pb_t_kernel(
         def regroup(c):
             s_lo, r_hi = s_parts_of[c]
             nc.scalar.copy(
-                out=s_grp_of[c][:, 0, :, :].rearrange("p (n i) t -> p n t i", i=RUN),
+                out=s_grp_of[c][0][:].rearrange("p (n i) t -> p n t i", i=RUN),
                 in_=s_lo[:].rearrange("p t (n i) -> p n t i", i=RUN),
             )
 
@@ -314,7 +315,7 @@ def tile_edgeupdaterwrapper_v01_pb_t_kernel(
                 nc.vector.quantize_mx(
                     out=s_codes[:, a, :].bitcast(FP8X4),
                     scales=s_scales[:, a, :],
-                    in_=s_grp_of[c][:, a, :, :].rearrange("p e t -> p (e t)"),
+                    in_=s_grp_of[c][a][:].rearrange("p e t -> p (e t)"),
                 )
             s_mx_of[c] = (s_codes, s_scales)
 
@@ -393,39 +394,40 @@ def tile_edgeupdaterwrapper_v01_pb_t_kernel(
                         stop=True,
                     )
                 q_banks.append(q_ps)
-            rstd = work.tile([P, TILES], F32)
-            nc.vector.reciprocal(out=rstd[:], in_=ln_of[c]["std"][:])
-            result = work.tile([P, TILES, EDGE_F], F32)
             ln_of[c]["q"] = q_banks
-            ln_of[c]["rstd"] = rstd
-            ln_of[c]["result"] = result
 
-        def normalise(c, b):
+        def centre_and_gain(c):
             zb = ln_of[c]["zb"]
             neg_mean = ln_of[c]["neg_mean"]
-            rstd = ln_of[c]["rstd"]
-            result = ln_of[c]["result"]
-            scaled = work.tile([P, 2, EDGE_F], F32)
-            for l in range(2):
-                n = 2 * b + l
+            rstd = work.tile([P, TILES], F32)
+            nc.vector.reciprocal(out=rstd[:], in_=ln_of[c]["std"][:])
+            scaled = work.tile([P, TILES, EDGE_F], F32)
+            for n in range(TILES):
                 nc.vector.scalar_tensor_tensor(
-                    out=scaled[:, l, :],
+                    out=scaled[:, n, :],
                     in0=zb[:, n, :],
                     scalar=neg_mean[:, n : n + 1],
                     in1=g_bc,
                     op0=ALU.add,
                     op1=ALU.mult,
                 )
-            for l in range(2):
-                n = 2 * b + l
+            ln_of[c]["rstd"] = rstd
+            ln_of[c]["scaled"] = scaled
+
+        def finish(c):
+            rstd = ln_of[c]["rstd"]
+            scaled = ln_of[c]["scaled"]
+            result = work.tile([P, TILES, EDGE_F], F32)
+            for n in range(TILES):
                 nc.vector.scalar_tensor_tensor(
                     out=result[:, n, :],
-                    in0=scaled[:, l, :],
+                    in0=scaled[:, n, :],
                     scalar=rstd[:, n : n + 1],
-                    in1=ln_of[c]["q"][b][:, l, :],
+                    in1=ln_of[c]["q"][n // 2][:, n % 2, :],
                     op0=ALU.mult,
                     op1=ALU.add,
                 )
+            ln_of[c]["result"] = result
 
         def store(c):
             nc.sync.dma_start(
@@ -436,27 +438,28 @@ def tile_edgeupdaterwrapper_v01_pb_t_kernel(
         def live(c):
             return 0 <= c < N_CHUNKS
 
-        for j in range(-1, N_CHUNKS + 3):
-            if live(j):
-                stage1(j)
-                add_z(nc.gpsimd, j, 1)
+        for j in range(-2, N_CHUNKS + 3):
+            if live(j - 3):
+                centre_and_gain(j - 3)
             if live(j + 1):
-                transposes(j + 1)
-            if live(j):
-                regroup(j)
-            if j == 0:
-                prepare_stage2()
+                quantise_hid(j + 1)
             if live(j - 1):
                 add_z(nc.vector, j - 1, 0)
                 quantise_s(j - 1)
-            if live(j + 1):
-                quantise_hid(j + 1)
             if live(j - 3):
                 residual(j - 3)
-                normalise(j - 3, 0)
-                normalise(j - 3, 1)
+                finish(j - 3)
                 store(j - 3)
-            if live(j - 1):
-                stage2(j - 1)
+            if live(j):
+                stage1(j)
+                add_z(nc.gpsimd, j, 1)
+            if j == 0:
+                prepare_stage2()
+            if live(j + 2):
+                transposes(j + 2)
             if live(j - 2):
                 variance(j - 2)
+            if live(j):
+                regroup(j)
+            if live(j - 1):
+                stage2(j - 1)

@@ -291,13 +291,12 @@ def tile_edgeupdaterwrapper_v01_pb_t_kernel(
                         op1=ALU.add,
                     )
 
-        def add_z(engine, c, b):
+        def add_z(c):
             s_lo, r_hi = s_parts_of[c]
-            edges = slice(HALF * b, HALF * (b + 1))
-            engine.tensor_tensor(
-                out=s_grp_of[c][1][:, edges, :],
-                in0=r_hi[:, :, edges].rearrange("p t e -> p e t"),
-                in1=z_grp_of[c][:].rearrange("p (e t) -> p e t", t=PACK)[:, edges, :],
+            nc.gpsimd.tensor_tensor(
+                out=s_grp_of[c][1][:],
+                in0=r_hi[:].rearrange("p t e -> p e t"),
+                in1=z_grp_of[c][:].rearrange("p (e t) -> p e t", t=PACK),
                 op=ALU.add,
             )
 
@@ -444,7 +443,6 @@ def tile_edgeupdaterwrapper_v01_pb_t_kernel(
             if live(j + 1):
                 quantise_hid(j + 1)
             if live(j - 1):
-                add_z(nc.vector, j - 1, 0)
                 quantise_s(j - 1)
             if live(j - 3):
                 residual(j - 3)
@@ -452,7 +450,7 @@ def tile_edgeupdaterwrapper_v01_pb_t_kernel(
                 store(j - 3)
             if live(j):
                 stage1(j)
-                add_z(nc.gpsimd, j, 1)
+                add_z(j)
             if j == 0:
                 prepare_stage2()
             if live(j + 2):

@@ -21,13 +21,11 @@ EDGE_F = 256
 MID = 2 * NODE_F + EDGE_F
 EPS = 1e-5
 
-CHUNK = 512
+CHUNK = 256
 N_CHUNKS = EDGES // CHUNK
 TILES = CHUNK // P
 ROWS_I = CHUNK // NODES
-PLANES = MID // P
-HALF = CHUNK // 2
-RUN = 4
+LOAD = 2
 
 FLOPS = 2 * EDGES * HID * MID + 2 * EDGES * MID * EDGE_F
 
@@ -55,58 +53,52 @@ def tile_edgeupdaterwrapper_v01_pb_t_kernel(
         nc.vector.memset(ones_bf[:], 1.0)
         eps_col = keep.tile([P, 1], F32)
         nc.vector.memset(eps_col[:], EPS)
-
-        xd2 = keep.tile([P, NODE_F], BF16)
-        nc.sync.dma_start(out=xd2[0:NODES, :], in_=xd)
-        nc.sync.dma_start(out=xd2[NODES:P, :], in_=xd)
-
-        b2_rows = keep.tile([P, P + HID], BF16)
-        nc.vector.memset(b2_rows[:], 0.0)
-        nc.sync.dma_start(out=b2_rows[0:4, 0:P], in_=b2[0:512].rearrange("(t c) -> t c", t=4))
-        b2_mixed = b2_rows[0:1, P : P + HID].rearrange("o (g k c) -> o g k c", g=2, k=2)
-        for k in range(2):
-            nc.sync.dma_start(
-                out=b2_mixed[:, :, k, :],
-                in_=b2[512 + 256 * k : 768 + 256 * k].rearrange("(o g c) -> o g c", o=1, g=2),
-            )
-
-        w2_raw = keep.tile([P, PACK, MID], BF16)
-        for u in range(2):
-            nc.sync.dma_start(
-                out=w2_raw[:, 2 * u : 2 * u + 2, :],
-                in_=W2[256 * u : 256 * u + 256, :].rearrange("(p h) f -> p h f", h=2),
-            )
+        warm = keep.tile([P, 1], F32)
+        nc.scalar.activation(out=warm[:], in_=eps_col[:], func=ACT.Sqrt, bias=0.0, scale=1.0)
 
         hid_sb = keep.tile([P, EDGES // P, HID], BF16)
         z_mixed = keep.tile([P, EDGES // P, HID], BF16)
         z_cols = z_mixed[:].rearrange("p T (g k c) -> p T g k c", g=2, k=2)
 
-        def load_hid(c):
+        def load_hid(c, n):
             nc.sync.dma_start(
-                out=hid_sb[:, TILES * c : TILES * (c + 1), :],
-                in_=hid_rows[CHUNK * c : CHUNK * (c + 1), :].rearrange("(T p) k -> p T k", p=P),
+                out=hid_sb[:, TILES * c : TILES * (c + n), :],
+                in_=hid_rows[CHUNK * c : CHUNK * (c + n), :].rearrange("(T p) k -> p T k", p=P),
             )
 
-        def load_p_ln(c2):
+        def load_p_ln(c, n):
             for g in range(2):
                 nc.sync.dma_start(
-                    out=z_cols[:, 2 * TILES * c2 : 2 * TILES * (c2 + 1), g, 1, :],
-                    in_=p_rows[2 * CHUNK * c2 : 2 * CHUNK * (c2 + 1), P * g : P * (g + 1)].rearrange(
+                    out=z_cols[:, TILES * c : TILES * (c + n), g, 1, :],
+                    in_=p_rows[CHUNK * c : CHUNK * (c + n), P * g : P * (g + 1)].rearrange(
                         "(T p) f -> p T f", p=P
                     ),
                 )
 
-        load_hid(0)
-        load_p_ln(0)
+        xd2 = keep.tile([P, NODE_F], BF16)
+        nc.sync.dma_start(out=xd2[0:NODES, :], in_=xd)
+        nc.sync.dma_start(out=xd2[NODES:P, :], in_=xd)
+        load_hid(0, 1)
 
-        wo_raw = keep.tile([P, 2, PACK, EDGE_F], BF16)
-        nc.sync.dma_start(out=wo_raw[:, 0, :, :], in_=Wo[0:512, :].rearrange("(t p) f -> p t f", p=P))
+        w2_raw = keep.tile([P, PACK, MID], BF16)
+        for a in range(2):
+            for u in range(2):
+                nc.sync.dma_start(
+                    out=w2_raw[:, 2 * u : 2 * u + 2, 512 * a : 512 * (a + 1)],
+                    in_=W2[256 * u : 256 * u + 256, 512 * a : 512 * (a + 1)].rearrange(
+                        "(p h) f -> p h f", h=2
+                    ),
+                )
+
+        b2_rows = keep.tile([P, P + HID], BF16)
+        nc.vector.memset(b2_rows[:], 0.0)
+        nc.gpsimd.dma_start(out=b2_rows[0:4, 0:P], in_=b2[0:512].rearrange("(t c) -> t c", t=4))
+        b2_mixed = b2_rows[0:1, P : P + HID].rearrange("o (g k c) -> o g k c", g=2, k=2)
         for k in range(2):
-            nc.sync.dma_start(
-                out=wo_raw[64 * k : 64 * k + 64, 1, :, :].rearrange("m (u h) f -> m u (h f)", h=2),
-                in_=Wo[512 + 256 * k : 768 + 256 * k, :].rearrange("(u m h) f -> m u (h f)", u=2, h=2),
+            nc.gpsimd.dma_start(
+                out=b2_mixed[:, :, k, :],
+                in_=b2[512 + 256 * k : 768 + 256 * k].rearrange("(o g c) -> o g c", o=1, g=2),
             )
-
         vec_rows = keep.tile([P, 3 * EDGE_F], BF16)
         nc.vector.memset(vec_rows[:], 0.0)
         for n, vec in enumerate((bo, ln_out_g, ln_out_b)):
@@ -115,130 +107,113 @@ def tile_edgeupdaterwrapper_v01_pb_t_kernel(
                 in_=vec.rearrange("(o f) -> o f", o=1),
             )
 
-        for c in range(1, N_CHUNKS):
-            load_hid(c)
-            if c % 2 == 0:
-                load_p_ln(c // 2)
+        load_hid(1, 1)
+        load_p_ln(0, LOAD)
 
-        for g in range(2):
-            nc.vector.tensor_copy(
-                out=z_cols[:, :, g, 0, :],
-                in_=xd2[:, P * (g + 1) : P * (g + 2)].unsqueeze(1).to_broadcast([P, EDGES // P, P]),
+        wo_raw = keep.tile([P, 2, PACK, EDGE_F], BF16)
+        nc.sync.dma_start(out=wo_raw[:, 0, :, :], in_=Wo[0:512, :].rearrange("(t p) f -> p t f", p=P))
+        for k in range(2):
+            nc.sync.dma_start(
+                out=wo_raw[64 * k : 64 * k + 64, 1, :, :].rearrange("m (u h) f -> m u (h f)", h=2),
+                in_=Wo[512 + 256 * k : 768 + 256 * k, :].rearrange("(u m h) f -> m u (h f)", u=2, h=2),
             )
+        for c in range(LOAD, N_CHUNKS, LOAD):
+            load_hid(c, LOAD)
+            load_p_ln(c, LOAD)
 
-        xt_ps = psum.tile([P, 4, P], BF16, tag="tr", bufs=2)
+        def fill_node_j(first, last):
+            for g in range(2):
+                nc.vector.tensor_copy(
+                    out=z_cols[:, first:last, g, 0, :],
+                    in_=xd2[:, P * (g + 1) : P * (g + 2)].unsqueeze(1).to_broadcast([P, last - first, P]),
+                )
+
+        fill_node_j(0, 2 * TILES)
+
+        xt_ps = psum.tile([P, 4, P], BF16, tag="q")
         for t in range(3):
             nc.tensor.transpose(xt_ps[:, t, :], xd2[:, P * t : P * (t + 1)], ident_bf[:])
         nc.tensor.transpose(xt_ps[:, 3, :], b2_rows[:, 0:P], ident_bf[:])
-        xt = keep.tile([P, 4, P], F32)
-        nc.vector.tensor_copy(out=xt[:], in_=xt_ps[:])
-
-        neg_b = keep.tile([P, 4], F32)
-        nc.vector.tensor_scalar(
-            out=neg_b[:], in0=xt[:, 3, 0:4], scalar1=-1.0, scalar2=None, op0=ALU.mult
-        )
-        b_plus_z = keep.tile([P, 4, NODES], F32)
-        for t in range(4):
-            nc.vector.tensor_scalar(
-                out=b_plus_z[:, t, :],
-                in0=xt[:, t % 3, 0:NODES],
-                scalar1=xt[:, 3, t : t + 1],
-                scalar2=None,
-                op0=ALU.add,
-            )
-
-        b2m_ps = psum.tile([P, 2, P], F32, tag="tr", bufs=2)
-        for u in range(2):
-            nc.tensor.transpose(
-                b2m_ps[:, u, :],
-                b2_rows[:, P : P + HID].bitcast(F32)[:, P * u : P * (u + 1)],
-                ident_f32[:],
-            )
-        b2_hi = keep.tile([P, 4], F32)
-        nc.vector.tensor_copy(
-            out=b2_hi[:].rearrange("p (u h) -> p u h", h=2),
-            in_=b2m_ps[:].bitcast(BF16).rearrange("p u (n h) -> p u n h", h=2)[:, :, 0, :],
-        )
+        x_words = keep.tile([P, NODES, PACK], BF16)
+        b2_lo = keep.tile([P, PACK], F32)
+        b2_hi = keep.tile([P, PACK], F32)
 
         w2_grp = keep.tile([P, MID, PACK], BF16, align_bytes=64)
         w2_codes = keep.tile([P, MID], U32, align_bytes=64)
         w2_scales = keep.tile([P, MID], U8, align_bytes=64)
-        nc.vector.tensor_copy(
-            out=w2_grp[:, 0:512, :], in_=w2_raw[:, :, 0:512].rearrange("p t f -> p f t")
-        )
         w2_hi = w2_raw[:, :, 512:1024].rearrange(
             "p t (k u m h) -> p u h k m t", k=2, u=2, m=64, h=2
         )
-        for u in range(2):
-            for h in range(2):
-                plane = 4 + 2 * u + h
-                nc.scalar.copy(
-                    out=w2_grp[:, P * plane : P * (plane + 1), :].rearrange(
-                        "p (k m) t -> p k m t", k=2
-                    ),
-                    in_=w2_hi[:, u, h],
-                )
-        for a in range(2):
+
+        def quantise_w2(a):
             nc.vector.quantize_mx(
                 out=w2_codes[:, 512 * a : 512 * (a + 1)].bitcast(FP8X4),
                 scales=w2_scales[:, 512 * a : 512 * (a + 1)],
                 in_=w2_grp[:, 512 * a : 512 * (a + 1), :].rearrange("p f t -> p (f t)"),
             )
 
+        def group_w2_hi(engine_copy, plane_t):
+            u, h = plane_t // 2, plane_t % 2
+            plane = 4 + plane_t
+            engine_copy(
+                out=w2_grp[:, P * plane : P * (plane + 1), :].rearrange("p (k m) t -> p k m t", k=2),
+                in_=w2_hi[:, u, h],
+            )
+
         wo_grp = keep.tile([P, 2, EDGE_F, PACK], BF16, align_bytes=64)
         wo_codes = keep.tile([P, 2 * EDGE_F], U32, align_bytes=64)
         wo_scales = keep.tile([P, 2 * EDGE_F], U8, align_bytes=64)
-        bo_g = keep.tile([P, 2 * EDGE_F], F32)
-        bo_bc = bo_g[:, 0:EDGE_F]
-        g_bc = bo_g[:, EDGE_F : 2 * EDGE_F]
+        bo_g = keep.tile([P, 2, EDGE_F], F32)
+        bo_bc = bo_g[:, 0, :]
+        g_bc = bo_g[:, 1, :]
 
         def prepare_stage2():
             for a in range(2):
                 nc.vector.tensor_copy(
                     out=wo_grp[:, a, :, :], in_=wo_raw[:, a, :, :].rearrange("p t f -> p f t")
                 )
+            bc_ps = psum.tile([P, 2 * EDGE_F], F32, tag="q")
+            nc.tensor.matmul(
+                bc_ps[:], lhsT=ones_bf[:], rhs=vec_rows[:, 0 : 2 * EDGE_F], start=True, stop=True
+            )
+            nc.vector.tensor_copy(out=bo_g[:].rearrange("p a f -> p (a f)"), in_=bc_ps[:])
             nc.vector.quantize_mx(
                 out=wo_codes[:].bitcast(FP8X4),
                 scales=wo_scales[:],
                 in_=wo_grp[:].rearrange("p a f t -> p (a f t)"),
             )
-            bc_ps = psum.tile([P, 2 * EDGE_F], F32, tag="h1", bufs=4)
-            nc.tensor.matmul(
-                bc_ps[:], lhsT=ones_bf[:], rhs=vec_rows[:, 0 : 2 * EDGE_F], start=True, stop=True
-            )
-            nc.vector.tensor_copy(out=bo_g[:], in_=bc_ps[:])
 
         hid_grp_of = {}
-        z_grp_of = {}
+        z_words_of = {}
         hid_mx_of = {}
-        s_parts_of = {}
+        r_of = {}
         s_grp_of = {}
         s_mx_of = {}
         ln_of = {}
 
-        def transpose_words(rows, c, grouped):
-            words = grouped[:].bitcast(F32).rearrange("p (e u) -> p e u", u=2)
-            for b in range(2):
-                words_t = psum.tile([P, 2, HALF], F32, tag="tr", bufs=2)
-                for u in range(2):
-                    for l in range(2):
-                        nc.tensor.transpose(
-                            words_t[:, u, P * l : P * (l + 1)],
-                            rows[:, TILES * c + 2 * b + l, :].bitcast(F32)[:, P * u : P * (u + 1)],
-                            ident_f32[:],
-                        )
-                nc.scalar.copy(
-                    out=words[:, HALF * b : HALF * (b + 1), :],
-                    in_=words_t[:].rearrange("p u e -> p e u"),
-                )
+        def transpose_words(rows, c, words_t):
+            for u in range(2):
+                for l in range(TILES):
+                    nc.tensor.transpose(
+                        words_t[:, u, P * l : P * (l + 1)],
+                        rows[:, TILES * c + l, :].bitcast(F32)[:, P * u : P * (u + 1)],
+                        ident_f32[:],
+                    )
 
-        def transposes(c):
-            hid_grp = work.tile([P, CHUNK * PACK], BF16, align_bytes=64, bufs=2)
-            transpose_words(hid_sb, c, hid_grp)
+        def bring_hid(c):
+            words_t = psum.tile([P, 2, CHUNK], F32, tag="hid_t")
+            transpose_words(hid_sb, c, words_t)
+            hid_grp = work.tile([P, CHUNK * PACK], BF16, align_bytes=64, bufs=3)
+            nc.scalar.copy(
+                out=hid_grp[:].bitcast(F32).rearrange("p (e u) -> p e u", u=2),
+                in_=words_t[:].rearrange("p u e -> p e u"),
+            )
             hid_grp_of[c] = hid_grp
-            z_grp = work.tile([P, CHUNK * PACK], BF16, bufs=4)
-            transpose_words(z_mixed, c, z_grp)
-            z_grp_of[c] = z_grp
+
+        def bring_z(c):
+            words_t = psum.tile([P, 2, CHUNK], F32, tag="z_t")
+            transpose_words(z_mixed, c, words_t)
+            z_words_of[c] = words_t
 
         def quantise_hid(c):
             hid_codes = work.tile([P, CHUNK], U32, align_bytes=64)
@@ -250,112 +225,105 @@ def tile_edgeupdaterwrapper_v01_pb_t_kernel(
 
         def stage1(c):
             hid_codes, hid_scales = hid_mx_of[c]
-            s_lo = work.tile([P, PACK, CHUNK], BF16)
+            r_lo = work.tile([P, PACK, CHUNK], F32)
             r_hi = work.tile([P, PACK, CHUNK], F32)
-            s_parts_of[c] = (s_lo, r_hi)
-            s_grp_lo = work.tile([P, CHUNK, PACK], BF16, align_bytes=64)
-            s_grp_hi = work.tile([P, CHUNK, PACK], BF16, align_bytes=64, bufs=1)
-            s_grp_of[c] = (s_grp_lo, s_grp_hi)
-            for a in (1, 0):
-                for t in range(PACK):
-                    plane = PACK * a + t
-                    h1 = psum.tile([P, CHUNK], F32, tag="h1", bufs=4)
-                    nc.tensor.matmul_mx(
-                        out=h1[:],
-                        lhsT=w2_codes[:, P * plane : P * (plane + 1)].bitcast(FP8X4),
-                        lhsT_scale=w2_scales[:, P * plane : P * (plane + 1)],
-                        rhs=hid_codes[:].bitcast(FP8X4),
-                        rhs_scale=hid_scales[:],
-                        start=True,
-                        stop=True,
-                    )
-                    if a == 1:
+            r_of[c] = (r_lo, r_hi)
+            for r, bias, first_plane in ((r_lo, b2_lo, 0), (r_hi, b2_hi, PACK)):
+                for pair in range(2):
+                    h1 = psum.tile([P, 2, CHUNK], F32, tag="h1", bufs=4)
+                    for l in range(2):
+                        plane = first_plane + 2 * pair + l
+                        nc.tensor.matmul_mx(
+                            out=h1[:, l, :],
+                            lhsT=w2_codes[:, P * plane : P * (plane + 1)].bitcast(FP8X4),
+                            lhsT_scale=w2_scales[:, P * plane : P * (plane + 1)],
+                            rhs=hid_codes[:].bitcast(FP8X4),
+                            rhs_scale=hid_scales[:],
+                            start=True,
+                            stop=True,
+                        )
+                    for l in range(2):
+                        t = 2 * pair + l
                         nc.scalar.activation(
-                            out=r_hi[:, t, :], in_=h1[:], func=ACT.Relu, bias=b2_hi[:, t : t + 1], scale=1.0
+                            out=r[:, t, :], in_=h1[:, l, :], func=ACT.Relu, bias=bias[:, t : t + 1], scale=1.0
                         )
-                        continue
-                    if t < 3:
-                        z_view = (
-                            b_plus_z[:, t, ROWS_I * c : ROWS_I * (c + 1)]
-                            .unsqueeze(2)
-                            .to_broadcast([P, ROWS_I, NODES])
-                        )
-                    else:
-                        z_view = b_plus_z[:, t, :].unsqueeze(1).to_broadcast([P, ROWS_I, NODES])
-                    nc.vector.scalar_tensor_tensor(
-                        out=s_lo[:, t, :].rearrange("p (i j) -> p i j", j=NODES),
-                        in0=h1[:].rearrange("p (i j) -> p i j", j=NODES),
-                        scalar=neg_b[:, t : t + 1],
-                        in1=z_view,
-                        op0=ALU.max,
-                        op1=ALU.add,
-                    )
 
-        def add_z(c):
-            s_lo, r_hi = s_parts_of[c]
+        def add_nodes(c):
+            r_lo = r_of[c][0][:].rearrange("p t (i j) -> p i j t", j=NODES)
+            s_lo = work.tile([P, CHUNK, PACK], BF16, align_bytes=64, bufs=1)
+            s_lo_view = s_lo[:].rearrange("p (i j) t -> p i j t", j=NODES)
             nc.gpsimd.tensor_tensor(
-                out=s_grp_of[c][1][:],
-                in0=r_hi[:].rearrange("p t e -> p e t"),
-                in1=z_grp_of[c][:].rearrange("p (e t) -> p e t", t=PACK),
+                out=s_lo_view[:, :, :, 0:3],
+                in0=r_lo[:, :, :, 0:3],
+                in1=x_words[:, ROWS_I * c : ROWS_I * (c + 1), 0:3]
+                .unsqueeze(2)
+                .to_broadcast([P, ROWS_I, NODES, 3]),
                 op=ALU.add,
             )
-
-        def regroup(c):
-            s_lo, r_hi = s_parts_of[c]
-            nc.scalar.copy(
-                out=s_grp_of[c][0][:].rearrange("p (n i) t -> p n t i", i=RUN),
-                in_=s_lo[:].rearrange("p t (n i) -> p n t i", i=RUN),
+            nc.gpsimd.tensor_tensor(
+                out=s_lo_view[:, :, :, 3],
+                in0=r_lo[:, :, :, 3],
+                in1=x_words[:, :, 0].unsqueeze(1).to_broadcast([P, ROWS_I, NODES]),
+                op=ALU.add,
             )
+            s_grp_of[c, 0] = s_lo
 
-        def quantise_s(c):
-            s_codes = work.tile([P, 2, CHUNK], U32, align_bytes=64)
-            s_scales = work.tile([P, 2, CHUNK], U8, align_bytes=64)
-            for a in range(2):
-                nc.vector.quantize_mx(
-                    out=s_codes[:, a, :].bitcast(FP8X4),
-                    scales=s_scales[:, a, :],
-                    in_=s_grp_of[c][a][:].rearrange("p e t -> p (e t)"),
-                )
-            s_mx_of[c] = (s_codes, s_scales)
+        def add_z(c):
+            s_hi = work.tile([P, CHUNK, PACK], BF16, align_bytes=64)
+            nc.vector.tensor_tensor(
+                out=s_hi[:].rearrange("p e (u h) -> p e u h", h=2),
+                in0=r_of[c][1][:].rearrange("p (u h) e -> p e u h", h=2),
+                in1=z_words_of[c][:].bitcast(BF16).rearrange("p u (e h) -> p e u h", h=2),
+                op=ALU.add,
+            )
+            s_grp_of[c, 1] = s_hi
+
+        def quantise_s(c, a):
+            s_codes = work.tile([P, CHUNK], U32, align_bytes=64, bufs=4)
+            s_scales = work.tile([P, CHUNK], U8, align_bytes=64, bufs=4)
+            nc.vector.quantize_mx(
+                out=s_codes[:].bitcast(FP8X4),
+                scales=s_scales[:],
+                in_=s_grp_of[c, a][:].rearrange("p e t -> p (e t)"),
+            )
+            s_mx_of[c, a] = (s_codes, s_scales)
 
         def stage2(c):
-            s_codes, s_scales = s_mx_of[c]
-            zb = work.tile([P, TILES, EDGE_F], F32, bufs=3)
-            row_sum = work.tile([P, TILES], F32)
-            neg_mean = work.tile([P, TILES], F32, bufs=4)
-            for b in range(2):
-                z2 = psum.tile([P, 2, EDGE_F], F32, tag="ln", bufs=2)
-                for l in range(2):
-                    n = 2 * b + l
-                    for a in range(2):
-                        nc.tensor.matmul_mx(
-                            out=z2[:, l, :],
-                            lhsT=s_codes[:, a, P * n : P * (n + 1)].bitcast(FP8X4),
-                            lhsT_scale=s_scales[:, a, P * n : P * (n + 1)],
-                            rhs=wo_codes[:, EDGE_F * a : EDGE_F * (a + 1)].bitcast(FP8X4),
-                            rhs_scale=wo_scales[:, EDGE_F * a : EDGE_F * (a + 1)],
-                            start=(a == 0),
-                            stop=(a == 1),
-                        )
-                for l in range(2):
-                    n = 2 * b + l
-                    nc.vector.scalar_tensor_tensor(
-                        out=zb[:, n, :],
-                        in0=z2[:, l, :],
-                        scalar=1.0,
-                        in1=bo_bc,
-                        op0=ALU.mult,
-                        op1=ALU.add,
-                        accum_out=row_sum[:, n : n + 1],
+            z2 = psum.tile([P, TILES, EDGE_F], F32, tag="z2")
+            for n in range(TILES):
+                for a in range(2):
+                    s_codes, s_scales = s_mx_of[c, a]
+                    nc.tensor.matmul_mx(
+                        out=z2[:, n, :],
+                        lhsT=s_codes[:, P * n : P * (n + 1)].bitcast(FP8X4),
+                        lhsT_scale=s_scales[:, P * n : P * (n + 1)],
+                        rhs=wo_codes[:, EDGE_F * a : EDGE_F * (a + 1)].bitcast(FP8X4),
+                        rhs_scale=wo_scales[:, EDGE_F * a : EDGE_F * (a + 1)],
+                        start=(a == 0),
+                        stop=(a == 1),
                     )
-            nc.vector.tensor_scalar(
-                out=neg_mean[:], in0=row_sum[:], scalar1=-1.0 / EDGE_F, scalar2=None, op0=ALU.mult
-            )
-            ln_of[c] = {"zb": zb, "neg_mean": neg_mean}
+            ln_of[c] = {"z2": z2}
 
-        def variance(c):
+        def add_bo(c):
+            zb = work.tile([P, TILES, EDGE_F], F32, bufs=4)
+            row_sum = work.tile([P, TILES], F32, bufs=4)
+            for n in range(TILES):
+                nc.vector.scalar_tensor_tensor(
+                    out=zb[:, n, :],
+                    in0=ln_of[c]["z2"][:, n, :],
+                    scalar=1.0,
+                    in1=bo_bc,
+                    op0=ALU.mult,
+                    op1=ALU.add,
+                    accum_out=row_sum[:, n : n + 1],
+                )
+            ln_of[c]["zb"] = zb
+            ln_of[c]["row_sum"] = row_sum
+
+        def statistics(c):
             zb = ln_of[c]["zb"]
-            neg_mean = ln_of[c]["neg_mean"]
+            neg_mean = work.tile([P, TILES], F32, bufs=4)
+            nc.scalar.mul(neg_mean[:], ln_of[c]["row_sum"][:], -1.0 / EDGE_F)
             squares = work.tile([P, TILES, EDGE_F], BF16)
             sq_sum = work.tile([P, TILES], F32)
             std = work.tile([P, TILES], F32, bufs=3)
@@ -372,40 +340,36 @@ def tile_edgeupdaterwrapper_v01_pb_t_kernel(
                 out=std[:], in_=sq_sum[:], func=ACT.Sqrt, bias=eps_col[:], scale=1.0 / EDGE_F
             )
             ln_of[c]["std"] = std
+            ln_of[c]["neg_mean"] = neg_mean
 
         def residual(c):
-            q_banks = []
-            for b in range(2):
-                q_ps = psum.tile([P, 2, EDGE_F], F32, tag="ln", bufs=2)
-                for l in range(2):
-                    nc.tensor.matmul(
-                        q_ps[:, l, :].rearrange("p (g f) -> p g f", g=2),
-                        lhsT=ident_bf[:],
-                        rhs=z_cols[:, TILES * c + 2 * b + l, :, 1, :],
-                        start=True,
-                        stop=False,
-                    )
-                    nc.tensor.matmul(
-                        q_ps[:, l, :],
-                        lhsT=ones_bf[:],
-                        rhs=vec_rows[:, 2 * EDGE_F : 3 * EDGE_F],
-                        start=False,
-                        stop=True,
-                    )
-                q_banks.append(q_ps)
-            ln_of[c]["q"] = q_banks
+            q = psum.tile([P, TILES, EDGE_F], F32, tag="q")
+            for n in range(TILES):
+                nc.tensor.matmul(
+                    q[:, n, :].rearrange("p (g f) -> p g f", g=2),
+                    lhsT=ident_bf[:],
+                    rhs=z_cols[:, TILES * c + n, :, 1, :],
+                    start=True,
+                    stop=False,
+                )
+                nc.tensor.matmul(
+                    q[:, n, :],
+                    lhsT=ones_bf[:],
+                    rhs=vec_rows[:, 2 * EDGE_F : 3 * EDGE_F],
+                    start=False,
+                    stop=True,
+                )
+            ln_of[c]["q"] = q
 
         def centre_and_gain(c):
-            zb = ln_of[c]["zb"]
-            neg_mean = ln_of[c]["neg_mean"]
             rstd = work.tile([P, TILES], F32)
             nc.vector.reciprocal(out=rstd[:], in_=ln_of[c]["std"][:])
             scaled = work.tile([P, TILES, EDGE_F], F32)
             for n in range(TILES):
                 nc.vector.scalar_tensor_tensor(
                     out=scaled[:, n, :],
-                    in0=zb[:, n, :],
-                    scalar=neg_mean[:, n : n + 1],
+                    in0=ln_of[c]["zb"][:, n, :],
+                    scalar=ln_of[c]["neg_mean"][:, n : n + 1],
                     in1=g_bc,
                     op0=ALU.add,
                     op1=ALU.mult,
@@ -414,50 +378,78 @@ def tile_edgeupdaterwrapper_v01_pb_t_kernel(
             ln_of[c]["scaled"] = scaled
 
         def finish(c):
-            rstd = ln_of[c]["rstd"]
-            scaled = ln_of[c]["scaled"]
-            result = work.tile([P, TILES, EDGE_F], F32)
+            result = work.tile([P, TILES, EDGE_F], F32, bufs=3)
             for n in range(TILES):
                 nc.vector.scalar_tensor_tensor(
                     out=result[:, n, :],
-                    in0=scaled[:, n, :],
-                    scalar=rstd[:, n : n + 1],
-                    in1=ln_of[c]["q"][n // 2][:, n % 2, :],
+                    in0=ln_of[c]["scaled"][:, n, :],
+                    scalar=ln_of[c]["rstd"][:, n : n + 1],
+                    in1=ln_of[c]["q"][:, n, :],
                     op0=ALU.mult,
                     op1=ALU.add,
                 )
-            ln_of[c]["result"] = result
-
-        def store(c):
             nc.sync.dma_start(
                 out=out_rows[CHUNK * c : CHUNK * (c + 1), :].rearrange("(T p) f -> p T f", p=P),
-                in_=ln_of[c]["result"][:],
+                in_=result[:],
             )
 
         def live(c):
             return 0 <= c < N_CHUNKS
 
-        for j in range(-2, N_CHUNKS + 3):
-            if live(j - 3):
-                centre_and_gain(j - 3)
+        bring_hid(0)
+        nc.vector.tensor_copy(out=w2_grp[:, 0:512, :], in_=w2_raw[:, :, 0:512].rearrange("p t f -> p f t"))
+        quantise_hid(0)
+        quantise_w2(0)
+        b2m_ps = psum.tile([P, 2, P], F32, tag="z2")
+        for u in range(2):
+            nc.tensor.transpose(
+                b2m_ps[:, u, :],
+                b2_rows[:, P : P + HID].bitcast(F32)[:, P * u : P * (u + 1)],
+                ident_f32[:],
+            )
+        nc.scalar.copy(out=b2_lo[:], in_=xt_ps[:, 3, 0:4])
+        nc.scalar.copy(
+            out=b2_hi[:].rearrange("p (u h) -> p u h", h=2),
+            in_=b2m_ps[:].bitcast(BF16).rearrange("p u (n h) -> p u n h", h=2)[:, :, 0, :],
+        )
+        bring_hid(1)
+        for plane_t in (2, 3):
+            group_w2_hi(nc.scalar.copy, plane_t)
+        for plane_t in (0, 1):
+            group_w2_hi(nc.vector.tensor_copy, plane_t)
+        quantise_w2(1)
+        nc.vector.tensor_copy(
+            out=x_words[:, :, 0:3], in_=xt_ps[:, 0:3, 0:NODES].rearrange("p t n -> p n t")
+        )
+
+        for j in range(N_CHUNKS + 3):
             if live(j + 1):
                 quantise_hid(j + 1)
             if live(j - 1):
-                quantise_s(j - 1)
+                quantise_s(j - 1, 1)
             if live(j - 3):
-                residual(j - 3)
-                finish(j - 3)
-                store(j - 3)
+                centre_and_gain(j - 3)
+            if live(j - 1):
+                quantise_s(j - 1, 0)
             if live(j):
                 stage1(j)
-                add_z(j)
+                add_nodes(j)
             if j == 0:
                 prepare_stage2()
-            if live(j + 2):
-                transposes(j + 2)
-            if live(j - 2):
-                variance(j - 2)
+                fill_node_j(2 * TILES, EDGES // P)
+            if live(j - 3):
+                residual(j - 3)
             if live(j):
-                regroup(j)
+                bring_z(j)
+            if live(j + 2):
+                bring_hid(j + 2)
             if live(j - 1):
                 stage2(j - 1)
+            if live(j - 2):
+                statistics(j - 2)
+            if live(j - 3):
+                finish(j - 3)
+            if live(j - 1):
+                add_bo(j - 1)
+            if live(j):
+                add_z(j)

@@ -21,11 +21,12 @@ EDGE_F = 256
 MID = 2 * NODE_F + EDGE_F
 EPS = 1e-5
 
-CHUNK = 256
-N_CHUNKS = EDGES // CHUNK
-TILES = CHUNK // P
-ROWS_I = CHUNK // NODES
-LOAD = 2
+CHUNK_TILES = [2] * 15 + [1] * 2
+N_CHUNKS = len(CHUNK_TILES)
+FIRST_TILE = [sum(CHUNK_TILES[:c]) for c in range(N_CHUNKS)]
+ALL_TILES = EDGES // P
+ROWS_TILE = P // NODES
+LOAD = 4
 
 FLOPS = 2 * EDGES * HID * MID + 2 * EDGES * MID * EDGE_F
 
@@ -49,39 +50,37 @@ def tile_edgeupdaterwrapper_v01_pb_t_kernel(
         ident_bf = keep.tile([P, P], BF16)
         make_identity(nc, ident_bf[:])
         ctx.enter_context(tc.manual_schedule())
-        ones_bf = keep.tile([P, P], BF16)
-        nc.vector.memset(ones_bf[:], 1.0)
+        b2_rows = keep.tile([P, P + HID], BF16)
+        nc.vector.memset(b2_rows[:], 0.0)
         eps_col = keep.tile([P, 1], F32)
         nc.vector.memset(eps_col[:], EPS)
-        warm = keep.tile([P, 1], F32)
-        nc.scalar.activation(out=warm[:], in_=eps_col[:], func=ACT.Sqrt, bias=0.0, scale=1.0)
+        vec_rows = keep.tile([P, 3 * EDGE_F], BF16)
+        nc.vector.memset(vec_rows[:], 0.0)
+        ones_bf = keep.tile([P, P], BF16)
+        nc.vector.memset(ones_bf[:], 1.0)
+        x_words = keep.tile([P, NODES, PACK], BF16)
+        nc.vector.memset(x_words[:], 0.0)
 
-        hid_sb = keep.tile([P, EDGES // P, HID], BF16)
-        z_mixed = keep.tile([P, EDGES // P, HID], BF16)
+        hid_sb = keep.tile([P, ALL_TILES, HID], BF16)
+        z_mixed = keep.tile([P, ALL_TILES, HID], BF16)
         z_cols = z_mixed[:].rearrange("p T (g k c) -> p T g k c", g=2, k=2)
 
-        def load_hid(c, n):
+        def load_hid(first, last):
             nc.sync.dma_start(
-                out=hid_sb[:, TILES * c : TILES * (c + n), :],
-                in_=hid_rows[CHUNK * c : CHUNK * (c + n), :].rearrange("(T p) k -> p T k", p=P),
+                out=hid_sb[:, first:last, :],
+                in_=hid_rows[P * first : P * last, :].rearrange("(T p) k -> p T k", p=P),
             )
 
-        def load_p_ln(c, n):
+        def load_p_ln(first, last):
             for g in range(2):
                 nc.sync.dma_start(
-                    out=z_cols[:, TILES * c : TILES * (c + n), g, 1, :],
-                    in_=p_rows[CHUNK * c : CHUNK * (c + n), P * g : P * (g + 1)].rearrange(
-                        "(T p) f -> p T f", p=P
-                    ),
+                    out=z_cols[:, first:last, g, 1, :],
+                    in_=p_rows[P * first : P * last, P * g : P * (g + 1)].rearrange("(T p) f -> p T f", p=P),
                 )
 
-        xd2 = keep.tile([P, NODE_F], BF16)
-        nc.sync.dma_start(out=xd2[0:NODES, :], in_=xd)
-        nc.sync.dma_start(out=xd2[NODES:P, :], in_=xd)
-        load_hid(0, 1)
-
         w2_raw = keep.tile([P, PACK, MID], BF16)
-        for a in range(2):
+
+        def load_w2(a):
             for u in range(2):
                 nc.sync.dma_start(
                     out=w2_raw[:, 2 * u : 2 * u + 2, 512 * a : 512 * (a + 1)],
@@ -90,25 +89,31 @@ def tile_edgeupdaterwrapper_v01_pb_t_kernel(
                     ),
                 )
 
-        b2_rows = keep.tile([P, P + HID], BF16)
-        nc.vector.memset(b2_rows[:], 0.0)
-        nc.gpsimd.dma_start(out=b2_rows[0:4, 0:P], in_=b2[0:512].rearrange("(t c) -> t c", t=4))
+        xd2 = keep.tile([P, NODE_F], BF16)
+        load_hid(0, 2)
+        load_w2(0)
+        nc.sync.dma_start(out=xd2[0:NODES, :], in_=xd)
+        nc.sync.dma_start(out=xd2[NODES:P, :], in_=xd)
+        load_w2(1)
+        load_hid(2, 4)
+        load_p_ln(0, LOAD)
+
+        nc.scalar.dma_start(out=b2_rows[0:4, 0:P], in_=b2[0:512].rearrange("(t c) -> t c", t=4))
         b2_mixed = b2_rows[0:1, P : P + HID].rearrange("o (g k c) -> o g k c", g=2, k=2)
         for k in range(2):
-            nc.gpsimd.dma_start(
+            nc.scalar.dma_start(
                 out=b2_mixed[:, :, k, :],
                 in_=b2[512 + 256 * k : 768 + 256 * k].rearrange("(o g c) -> o g c", o=1, g=2),
             )
-        vec_rows = keep.tile([P, 3 * EDGE_F], BF16)
-        nc.vector.memset(vec_rows[:], 0.0)
         for n, vec in enumerate((bo, ln_out_g, ln_out_b)):
             nc.gpsimd.dma_start(
                 out=vec_rows[0:1, EDGE_F * n : EDGE_F * (n + 1)],
                 in_=vec.rearrange("(o f) -> o f", o=1),
             )
-
-        load_hid(1, 1)
-        load_p_ln(0, LOAD)
+        warm = keep.tile([P, 1], F32)
+        nc.scalar.activation(
+            out=warm[:], in_=eps_col[:], func=ACT.Abs_reciprocal_sqrt, bias=0.0, scale=1.0
+        )
 
         wo_raw = keep.tile([P, 2, PACK, EDGE_F], BF16)
         nc.sync.dma_start(out=wo_raw[:, 0, :, :], in_=Wo[0:512, :].rearrange("(t p) f -> p t f", p=P))
@@ -117,9 +122,9 @@ def tile_edgeupdaterwrapper_v01_pb_t_kernel(
                 out=wo_raw[64 * k : 64 * k + 64, 1, :, :].rearrange("m (u h) f -> m u (h f)", h=2),
                 in_=Wo[512 + 256 * k : 768 + 256 * k, :].rearrange("(u m h) f -> m u (h f)", u=2, h=2),
             )
-        for c in range(LOAD, N_CHUNKS, LOAD):
-            load_hid(c, LOAD)
-            load_p_ln(c, LOAD)
+        for first in range(LOAD, ALL_TILES, LOAD):
+            load_hid(first, first + LOAD)
+            load_p_ln(first, first + LOAD)
 
         def fill_node_j(first, last):
             for g in range(2):
@@ -128,15 +133,37 @@ def tile_edgeupdaterwrapper_v01_pb_t_kernel(
                     in_=xd2[:, P * (g + 1) : P * (g + 2)].unsqueeze(1).to_broadcast([P, last - first, P]),
                 )
 
-        fill_node_j(0, 2 * TILES)
-
-        xt_ps = psum.tile([P, 4, P], BF16, tag="q")
-        for t in range(3):
-            nc.tensor.transpose(xt_ps[:, t, :], xd2[:, P * t : P * (t + 1)], ident_bf[:])
-        nc.tensor.transpose(xt_ps[:, 3, :], b2_rows[:, 0:P], ident_bf[:])
-        x_words = keep.tile([P, NODES, PACK], BF16)
         b2_lo = keep.tile([P, PACK], F32)
         b2_hi = keep.tile([P, PACK], F32)
+        neg_b3 = keep.tile([P, 1], F32)
+        b3_plus_x = keep.tile([P, NODES], F32)
+
+        def node_tables():
+            xt_ps = psum.tile([P, 4, P], BF16, tag="q")
+            for t in range(3):
+                nc.tensor.transpose(xt_ps[:, t, :], xd2[:, P * t : P * (t + 1)], ident_bf[:])
+            nc.tensor.transpose(xt_ps[:, 3, :], b2_rows[:, 0:P], ident_bf[:])
+            b2m_ps = psum.tile([P, 2, P], F32, tag="z2")
+            for u in range(2):
+                nc.tensor.transpose(
+                    b2m_ps[:, u, :],
+                    b2_rows[:, P : P + HID].bitcast(F32)[:, P * u : P * (u + 1)],
+                    ident_f32[:],
+                )
+            nc.scalar.copy(out=b2_lo[:], in_=xt_ps[:, 3, 0:4])
+            nc.scalar.copy(
+                out=b2_hi[:].rearrange("p (u h) -> p u h", h=2),
+                in_=b2m_ps[:].bitcast(BF16).rearrange("p u (n h) -> p u n h", h=2)[:, :, 0, :],
+            )
+            nc.vector.tensor_scalar(
+                out=neg_b3[:], in0=b2_lo[:, 3:4], scalar1=-1.0, scalar2=None, op0=ALU.mult
+            )
+            nc.vector.tensor_scalar(
+                out=b3_plus_x[:], in0=xt_ps[:, 0, 0:NODES], scalar1=b2_lo[:, 3:4], scalar2=None, op0=ALU.add
+            )
+            nc.vector.tensor_copy(
+                out=x_words[:, :, 0:3], in_=xt_ps[:, 0:3, 0:NODES].rearrange("p t n -> p n t")
+            )
 
         w2_grp = keep.tile([P, MID, PACK], BF16, align_bytes=64)
         w2_codes = keep.tile([P, MID], U32, align_bytes=64)
@@ -191,19 +218,22 @@ def tile_edgeupdaterwrapper_v01_pb_t_kernel(
         s_mx_of = {}
         ln_of = {}
 
+        def width(c):
+            return P * CHUNK_TILES[c]
+
         def transpose_words(rows, c, words_t):
             for u in range(2):
-                for l in range(TILES):
+                for l in range(CHUNK_TILES[c]):
                     nc.tensor.transpose(
                         words_t[:, u, P * l : P * (l + 1)],
-                        rows[:, TILES * c + l, :].bitcast(F32)[:, P * u : P * (u + 1)],
+                        rows[:, FIRST_TILE[c] + l, :].bitcast(F32)[:, P * u : P * (u + 1)],
                         ident_f32[:],
                     )
 
         def bring_hid(c):
-            words_t = psum.tile([P, 2, CHUNK], F32, tag="hid_t")
+            words_t = psum.tile([P, 2, width(c)], F32, tag="hid_t")
             transpose_words(hid_sb, c, words_t)
-            hid_grp = work.tile([P, CHUNK * PACK], BF16, align_bytes=64, bufs=3)
+            hid_grp = work.tile([P, width(c) * PACK], BF16, align_bytes=64, bufs=3)
             nc.scalar.copy(
                 out=hid_grp[:].bitcast(F32).rearrange("p (e u) -> p e u", u=2),
                 in_=words_t[:].rearrange("p u e -> p e u"),
@@ -211,76 +241,91 @@ def tile_edgeupdaterwrapper_v01_pb_t_kernel(
             hid_grp_of[c] = hid_grp
 
         def bring_z(c):
-            words_t = psum.tile([P, 2, CHUNK], F32, tag="z_t")
+            words_t = psum.tile([P, 2, width(c)], F32, tag="z_t")
             transpose_words(z_mixed, c, words_t)
             z_words_of[c] = words_t
 
         def quantise_hid(c):
-            hid_codes = work.tile([P, CHUNK], U32, align_bytes=64)
-            hid_scales = work.tile([P, CHUNK], U8, align_bytes=64)
+            hid_codes = work.tile([P, width(c)], U32, align_bytes=64)
+            hid_scales = work.tile([P, width(c)], U8, align_bytes=64)
             nc.vector.quantize_mx(
                 out=hid_codes[:].bitcast(FP8X4), scales=hid_scales[:], in_=hid_grp_of[c][:]
             )
             hid_mx_of[c] = (hid_codes, hid_scales)
 
-        def stage1(c):
+        def stage1_pair(c, first_plane):
             hid_codes, hid_scales = hid_mx_of[c]
-            r_lo = work.tile([P, PACK, CHUNK], F32)
-            r_hi = work.tile([P, PACK, CHUNK], F32)
-            r_of[c] = (r_lo, r_hi)
-            for r, bias, first_plane in ((r_lo, b2_lo, 0), (r_hi, b2_hi, PACK)):
-                for pair in range(2):
-                    h1 = psum.tile([P, 2, CHUNK], F32, tag="h1", bufs=4)
-                    for l in range(2):
-                        plane = first_plane + 2 * pair + l
-                        nc.tensor.matmul_mx(
-                            out=h1[:, l, :],
-                            lhsT=w2_codes[:, P * plane : P * (plane + 1)].bitcast(FP8X4),
-                            lhsT_scale=w2_scales[:, P * plane : P * (plane + 1)],
-                            rhs=hid_codes[:].bitcast(FP8X4),
-                            rhs_scale=hid_scales[:],
-                            start=True,
-                            stop=True,
-                        )
-                    for l in range(2):
-                        t = 2 * pair + l
-                        nc.scalar.activation(
-                            out=r[:, t, :], in_=h1[:, l, :], func=ACT.Relu, bias=bias[:, t : t + 1], scale=1.0
-                        )
+            h1 = psum.tile([P, 2, width(c)], F32, tag="h1", bufs=4)
+            for l in range(2):
+                plane = first_plane + l
+                nc.tensor.matmul_mx(
+                    out=h1[:, l, :],
+                    lhsT=w2_codes[:, P * plane : P * (plane + 1)].bitcast(FP8X4),
+                    lhsT_scale=w2_scales[:, P * plane : P * (plane + 1)],
+                    rhs=hid_codes[:].bitcast(FP8X4),
+                    rhs_scale=hid_scales[:],
+                    start=True,
+                    stop=True,
+                )
+            return h1
+
+        def relu(c, a, t, h):
+            bias = (b2_lo, b2_hi)[a][:, t : t + 1]
+            nc.scalar.activation(out=r_of[c, a][:, t, :], in_=h, func=ACT.Relu, bias=bias, scale=1.0)
+
+        def stage1_planes_2_3(c):
+            r_lo = work.tile([P, PACK, width(c)], F32)
+            r_of[c, 0] = r_lo
+            h1 = stage1_pair(c, 2)
+            relu(c, 0, 2, h1[:, 0, :])
+            rows_i = ROWS_TILE * CHUNK_TILES[c]
+            nc.vector.scalar_tensor_tensor(
+                out=r_lo[:, 3, :].rearrange("p (i j) -> p i j", j=NODES),
+                in0=h1[:, 1, :].rearrange("p (i j) -> p i j", j=NODES),
+                scalar=neg_b3[:],
+                in1=b3_plus_x[:].unsqueeze(1).to_broadcast([P, rows_i, NODES]),
+                op0=ALU.max,
+                op1=ALU.add,
+            )
+
+        def stage1_rest(c):
+            h1 = stage1_pair(c, 0)
+            for l in range(2):
+                relu(c, 0, l, h1[:, l, :])
+            r_hi = work.tile([P, PACK, width(c)], F32)
+            r_of[c, 1] = r_hi
+            for pair in range(2):
+                h1 = stage1_pair(c, PACK + 2 * pair)
+                for l in range(2):
+                    relu(c, 1, 2 * pair + l, h1[:, l, :])
 
         def add_nodes(c):
-            r_lo = r_of[c][0][:].rearrange("p t (i j) -> p i j t", j=NODES)
-            s_lo = work.tile([P, CHUNK, PACK], BF16, align_bytes=64, bufs=1)
-            s_lo_view = s_lo[:].rearrange("p (i j) t -> p i j t", j=NODES)
+            rows_i = ROWS_TILE * CHUNK_TILES[c]
+            first_i = ROWS_TILE * FIRST_TILE[c]
+            s_lo = work.tile([P, width(c), PACK], BF16, align_bytes=64, bufs=1)
             nc.gpsimd.tensor_tensor(
-                out=s_lo_view[:, :, :, 0:3],
-                in0=r_lo[:, :, :, 0:3],
-                in1=x_words[:, ROWS_I * c : ROWS_I * (c + 1), 0:3]
+                out=s_lo[:].rearrange("p (i j) t -> p i j t", j=NODES),
+                in0=r_of[c, 0][:].rearrange("p t (i j) -> p i j t", j=NODES),
+                in1=x_words[:, first_i : first_i + rows_i, :]
                 .unsqueeze(2)
-                .to_broadcast([P, ROWS_I, NODES, 3]),
-                op=ALU.add,
-            )
-            nc.gpsimd.tensor_tensor(
-                out=s_lo_view[:, :, :, 3],
-                in0=r_lo[:, :, :, 3],
-                in1=x_words[:, :, 0].unsqueeze(1).to_broadcast([P, ROWS_I, NODES]),
+                .to_broadcast([P, rows_i, NODES, PACK]),
                 op=ALU.add,
             )
             s_grp_of[c, 0] = s_lo
 
         def add_z(c):
-            s_hi = work.tile([P, CHUNK, PACK], BF16, align_bytes=64)
+            s_hi = work.tile([P, width(c), PACK], BF16, align_bytes=64)
             nc.vector.tensor_tensor(
                 out=s_hi[:].rearrange("p e (u h) -> p e u h", h=2),
-                in0=r_of[c][1][:].rearrange("p (u h) e -> p e u h", h=2),
+                in0=r_of[c, 1][:].rearrange("p (u h) e -> p e u h", h=2),
                 in1=z_words_of[c][:].bitcast(BF16).rearrange("p u (e h) -> p e u h", h=2),
                 op=ALU.add,
             )
             s_grp_of[c, 1] = s_hi
 
         def quantise_s(c, a):
-            s_codes = work.tile([P, CHUNK], U32, align_bytes=64, bufs=4)
-            s_scales = work.tile([P, CHUNK], U8, align_bytes=64, bufs=4)
+            s_codes = work.tile([P, width(c)], U32, align_bytes=64, bufs=4)
+            s_scales = work.tile([P, width(c)], U8, align_bytes=64, bufs=4)
             nc.vector.quantize_mx(
                 out=s_codes[:].bitcast(FP8X4),
                 scales=s_scales[:],
@@ -289,8 +334,8 @@ def tile_edgeupdaterwrapper_v01_pb_t_kernel(
             s_mx_of[c, a] = (s_codes, s_scales)
 
         def stage2(c):
-            z2 = psum.tile([P, TILES, EDGE_F], F32, tag="z2")
-            for n in range(TILES):
+            z2 = psum.tile([P, CHUNK_TILES[c], EDGE_F], F32, tag="z2")
+            for n in range(CHUNK_TILES[c]):
                 for a in range(2):
                     s_codes, s_scales = s_mx_of[c, a]
                     nc.tensor.matmul_mx(
@@ -305,9 +350,9 @@ def tile_edgeupdaterwrapper_v01_pb_t_kernel(
             ln_of[c] = {"z2": z2}
 
         def add_bo(c):
-            zb = work.tile([P, TILES, EDGE_F], F32, bufs=4)
-            row_sum = work.tile([P, TILES], F32, bufs=4)
-            for n in range(TILES):
+            zb = work.tile([P, CHUNK_TILES[c], EDGE_F], F32, bufs=4)
+            row_sum = work.tile([P, CHUNK_TILES[c]], F32, bufs=4)
+            for n in range(CHUNK_TILES[c]):
                 nc.vector.scalar_tensor_tensor(
                     out=zb[:, n, :],
                     in0=ln_of[c]["z2"][:, n, :],
@@ -322,12 +367,12 @@ def tile_edgeupdaterwrapper_v01_pb_t_kernel(
 
         def statistics(c):
             zb = ln_of[c]["zb"]
-            neg_mean = work.tile([P, TILES], F32, bufs=4)
+            neg_mean = work.tile([P, CHUNK_TILES[c]], F32, bufs=4)
             nc.scalar.mul(neg_mean[:], ln_of[c]["row_sum"][:], -1.0 / EDGE_F)
-            squares = work.tile([P, TILES, EDGE_F], BF16)
-            sq_sum = work.tile([P, TILES], F32)
-            std = work.tile([P, TILES], F32, bufs=3)
-            for n in range(TILES):
+            squares = work.tile([P, CHUNK_TILES[c], EDGE_F], BF16)
+            sq_sum = work.tile([P, CHUNK_TILES[c]], F32)
+            rstd = work.tile([P, CHUNK_TILES[c]], F32, bufs=3)
+            for n in range(CHUNK_TILES[c]):
                 nc.scalar.activation(
                     out=squares[:, n, :],
                     in_=zb[:, n, :],
@@ -337,18 +382,18 @@ def tile_edgeupdaterwrapper_v01_pb_t_kernel(
                     accum_out=sq_sum[:, n : n + 1],
                 )
             nc.scalar.activation(
-                out=std[:], in_=sq_sum[:], func=ACT.Sqrt, bias=eps_col[:], scale=1.0 / EDGE_F
+                out=rstd[:], in_=sq_sum[:], func=ACT.Abs_reciprocal_sqrt, bias=eps_col[:], scale=1.0 / EDGE_F
             )
-            ln_of[c]["std"] = std
+            ln_of[c]["rstd"] = rstd
             ln_of[c]["neg_mean"] = neg_mean
 
         def residual(c):
-            q = psum.tile([P, TILES, EDGE_F], F32, tag="q")
-            for n in range(TILES):
+            q = psum.tile([P, CHUNK_TILES[c], EDGE_F], F32, tag="q")
+            for n in range(CHUNK_TILES[c]):
                 nc.tensor.matmul(
                     q[:, n, :].rearrange("p (g f) -> p g f", g=2),
                     lhsT=ident_bf[:],
-                    rhs=z_cols[:, TILES * c + n, :, 1, :],
+                    rhs=z_cols[:, FIRST_TILE[c] + n, :, 1, :],
                     start=True,
                     stop=False,
                 )
@@ -362,10 +407,8 @@ def tile_edgeupdaterwrapper_v01_pb_t_kernel(
             ln_of[c]["q"] = q
 
         def centre_and_gain(c):
-            rstd = work.tile([P, TILES], F32)
-            nc.vector.reciprocal(out=rstd[:], in_=ln_of[c]["std"][:])
-            scaled = work.tile([P, TILES, EDGE_F], F32)
-            for n in range(TILES):
+            scaled = work.tile([P, CHUNK_TILES[c], EDGE_F], F32)
+            for n in range(CHUNK_TILES[c]):
                 nc.vector.scalar_tensor_tensor(
                     out=scaled[:, n, :],
                     in0=ln_of[c]["zb"][:, n, :],
@@ -374,12 +417,11 @@ def tile_edgeupdaterwrapper_v01_pb_t_kernel(
                     op0=ALU.add,
                     op1=ALU.mult,
                 )
-            ln_of[c]["rstd"] = rstd
             ln_of[c]["scaled"] = scaled
 
         def finish(c):
-            result = work.tile([P, TILES, EDGE_F], F32, bufs=3)
-            for n in range(TILES):
+            result = work.tile([P, CHUNK_TILES[c], EDGE_F], F32, bufs=3)
+            for n in range(CHUNK_TILES[c]):
                 nc.vector.scalar_tensor_tensor(
                     out=result[:, n, :],
                     in0=ln_of[c]["scaled"][:, n, :],
@@ -389,7 +431,9 @@ def tile_edgeupdaterwrapper_v01_pb_t_kernel(
                     op1=ALU.add,
                 )
             nc.sync.dma_start(
-                out=out_rows[CHUNK * c : CHUNK * (c + 1), :].rearrange("(T p) f -> p T f", p=P),
+                out=out_rows[P * FIRST_TILE[c] : P * FIRST_TILE[c] + width(c), :].rearrange(
+                    "(T p) f -> p T f", p=P
+                ),
                 in_=result[:],
             )
 
@@ -400,29 +444,18 @@ def tile_edgeupdaterwrapper_v01_pb_t_kernel(
         nc.vector.tensor_copy(out=w2_grp[:, 0:512, :], in_=w2_raw[:, :, 0:512].rearrange("p t f -> p f t"))
         quantise_hid(0)
         quantise_w2(0)
-        b2m_ps = psum.tile([P, 2, P], F32, tag="z2")
-        for u in range(2):
-            nc.tensor.transpose(
-                b2m_ps[:, u, :],
-                b2_rows[:, P : P + HID].bitcast(F32)[:, P * u : P * (u + 1)],
-                ident_f32[:],
-            )
-        nc.scalar.copy(out=b2_lo[:], in_=xt_ps[:, 3, 0:4])
-        nc.scalar.copy(
-            out=b2_hi[:].rearrange("p (u h) -> p u h", h=2),
-            in_=b2m_ps[:].bitcast(BF16).rearrange("p u (n h) -> p u n h", h=2)[:, :, 0, :],
-        )
+        node_tables()
         bring_hid(1)
         for plane_t in (2, 3):
             group_w2_hi(nc.scalar.copy, plane_t)
         for plane_t in (0, 1):
             group_w2_hi(nc.vector.tensor_copy, plane_t)
         quantise_w2(1)
-        nc.vector.tensor_copy(
-            out=x_words[:, :, 0:3], in_=xt_ps[:, 0:3, 0:NODES].rearrange("p t n -> p n t")
-        )
+        fill_node_j(0, 4)
 
         for j in range(N_CHUNKS + 3):
+            if live(j):
+                stage1_planes_2_3(j)
             if live(j + 1):
                 quantise_hid(j + 1)
             if live(j - 1):
@@ -432,11 +465,11 @@ def tile_edgeupdaterwrapper_v01_pb_t_kernel(
             if live(j - 1):
                 quantise_s(j - 1, 0)
             if live(j):
-                stage1(j)
+                stage1_rest(j)
                 add_nodes(j)
             if j == 0:
                 prepare_stage2()
-                fill_node_j(2 * TILES, EDGES // P)
+                fill_node_j(4, ALL_TILES)
             if live(j - 3):
                 residual(j - 3)
             if live(j):

@@ -26,6 +26,7 @@ N_CHUNKS = len(CHUNK_TILES)
 FIRST_TILE = [sum(CHUNK_TILES[:c]) for c in range(N_CHUNKS)]
 ALL_TILES = EDGES // P
 ROWS_TILE = P // NODES
+RUN = 4
 LOAD = 4
 
 FLOPS = 2 * EDGES * HID * MID + 2 * EDGES * MID * EDGE_F
@@ -60,6 +61,7 @@ def tile_edgeupdaterwrapper_v01_pb_t_kernel(
         nc.vector.memset(ones_bf[:], 1.0)
         x_words = keep.tile([P, NODES, PACK], BF16)
         nc.vector.memset(x_words[:], 0.0)
+        x_runs = keep.tile([P, NODES, NODES // RUN, PACK], BF16)
 
         hid_sb = keep.tile([P, ALL_TILES, HID], BF16)
         z_mixed = keep.tile([P, ALL_TILES, HID], BF16)
@@ -132,6 +134,14 @@ def tile_edgeupdaterwrapper_v01_pb_t_kernel(
                     out=z_cols[:, first:last, g, 0, :],
                     in_=xd2[:, P * (g + 1) : P * (g + 2)].unsqueeze(1).to_broadcast([P, last - first, P]),
                 )
+
+        def fill_node_i(first, last):
+            nc.vector.tensor_copy(
+                out=x_runs[:, first:last, :, :],
+                in_=x_words[:, first:last, :]
+                .unsqueeze(2)
+                .to_broadcast([P, last - first, NODES // RUN, PACK]),
+            )
 
         b2_lo = keep.tile([P, PACK], F32)
         b2_hi = keep.tile([P, PACK], F32)
@@ -225,14 +235,14 @@ def tile_edgeupdaterwrapper_v01_pb_t_kernel(
             for u in range(2):
                 for l in range(CHUNK_TILES[c]):
                     nc.tensor.transpose(
-                        words_t[:, u, P * l : P * (l + 1)],
+                        words_t[u][:, P * l : P * (l + 1)],
                         rows[:, FIRST_TILE[c] + l, :].bitcast(F32)[:, P * u : P * (u + 1)],
                         ident_f32[:],
                     )
 
         def bring_hid(c):
             words_t = psum.tile([P, 2, width(c)], F32, tag="hid_t")
-            transpose_words(hid_sb, c, words_t)
+            transpose_words(hid_sb, c, [words_t[:, u, :] for u in range(2)])
             hid_grp = work.tile([P, width(c) * PACK], BF16, align_bytes=64, bufs=3)
             nc.scalar.copy(
                 out=hid_grp[:].bitcast(F32).rearrange("p (e u) -> p e u", u=2),
@@ -241,8 +251,8 @@ def tile_edgeupdaterwrapper_v01_pb_t_kernel(
             hid_grp_of[c] = hid_grp
 
         def bring_z(c):
-            words_t = psum.tile([P, 2, width(c)], F32, tag="z_t")
-            transpose_words(z_mixed, c, words_t)
+            words_t = psum.tile([P, width(c), 2], F32, tag="z_t")
+            transpose_words(z_mixed, c, [words_t[:, :, u] for u in range(2)])
             z_words_of[c] = words_t
 
         def quantise_hid(c):
@@ -300,15 +310,15 @@ def tile_edgeupdaterwrapper_v01_pb_t_kernel(
                     relu(c, 1, 2 * pair + l, h1[:, l, :])
 
         def add_nodes(c):
-            rows_i = ROWS_TILE * CHUNK_TILES[c]
-            first_i = ROWS_TILE * FIRST_TILE[c]
+            runs = width(c) // RUN
+            first_run = P * FIRST_TILE[c] // RUN
             s_lo = work.tile([P, width(c), PACK], BF16, align_bytes=64, bufs=1)
             nc.gpsimd.tensor_tensor(
-                out=s_lo[:].rearrange("p (i j) t -> p i j t", j=NODES),
-                in0=r_of[c, 0][:].rearrange("p t (i j) -> p i j t", j=NODES),
-                in1=x_words[:, first_i : first_i + rows_i, :]
-                .unsqueeze(2)
-                .to_broadcast([P, rows_i, NODES, PACK]),
+                out=s_lo[:].rearrange("p (n i) t -> p n t i", i=RUN),
+                in0=r_of[c, 0][:].rearrange("p t (n i) -> p n t i", i=RUN),
+                in1=x_runs[:].rearrange("p i n t -> p (i n) t")[:, first_run : first_run + runs, :]
+                .unsqueeze(3)
+                .to_broadcast([P, runs, PACK, RUN]),
                 op=ALU.add,
             )
             s_grp_of[c, 0] = s_lo
@@ -316,9 +326,9 @@ def tile_edgeupdaterwrapper_v01_pb_t_kernel(
         def add_z(c):
             s_hi = work.tile([P, width(c), PACK], BF16, align_bytes=64)
             nc.vector.tensor_tensor(
-                out=s_hi[:].rearrange("p e (u h) -> p e u h", h=2),
-                in0=r_of[c, 1][:].rearrange("p (u h) e -> p e u h", h=2),
-                in1=z_words_of[c][:].bitcast(BF16).rearrange("p u (e h) -> p e u h", h=2),
+                out=s_hi[:].rearrange("p (n i) t -> p n t i", i=RUN),
+                in0=r_of[c, 1][:].rearrange("p t (n i) -> p n t i", i=RUN),
+                in1=z_words_of[c][:].bitcast(BF16).rearrange("p (n i) t -> p n t i", i=RUN),
                 op=ALU.add,
             )
             s_grp_of[c, 1] = s_hi
@@ -452,6 +462,7 @@ def tile_edgeupdaterwrapper_v01_pb_t_kernel(
             group_w2_hi(nc.vector.tensor_copy, plane_t)
         quantise_w2(1)
         fill_node_j(0, 4)
+        fill_node_i(0, 8)
 
         for j in range(N_CHUNKS + 3):
             if live(j):
@@ -467,9 +478,6 @@ def tile_edgeupdaterwrapper_v01_pb_t_kernel(
             if live(j):
                 stage1_rest(j)
                 add_nodes(j)
-            if j == 0:
-                prepare_stage2()
-                fill_node_j(4, ALL_TILES)
             if live(j - 3):
                 residual(j - 3)
             if live(j):
@@ -486,3 +494,9 @@ def tile_edgeupdaterwrapper_v01_pb_t_kernel(
                 add_bo(j - 1)
             if live(j):
                 add_z(j)
+            if j == 0:
+                prepare_stage2()
+                fill_node_j(4, 8)
+            if j == 1:
+                fill_node_i(8, NODES)
+                fill_node_j(8, ALL_TILES)

@@ -61,7 +61,6 @@ def tile_edgeupdaterwrapper_v01_pb_t_kernel(
         nc.vector.memset(ones_bf[:], 1.0)
         x_words = keep.tile([P, NODES, PACK], BF16)
         nc.vector.memset(x_words[:], 0.0)
-        x_runs = keep.tile([P, NODES, NODES // RUN, PACK], BF16)
 
         hid_sb = keep.tile([P, ALL_TILES, HID], BF16)
         z_mixed = keep.tile([P, ALL_TILES, HID], BF16)
@@ -134,14 +133,6 @@ def tile_edgeupdaterwrapper_v01_pb_t_kernel(
                     out=z_cols[:, first:last, g, 0, :],
                     in_=xd2[:, P * (g + 1) : P * (g + 2)].unsqueeze(1).to_broadcast([P, last - first, P]),
                 )
-
-        def fill_node_i(first, last):
-            nc.vector.tensor_copy(
-                out=x_runs[:, first:last, :, :],
-                in_=x_words[:, first:last, :]
-                .unsqueeze(2)
-                .to_broadcast([P, last - first, NODES // RUN, PACK]),
-            )
 
         b2_lo = keep.tile([P, PACK], F32)
         b2_hi = keep.tile([P, PACK], F32)
@@ -310,15 +301,15 @@ def tile_edgeupdaterwrapper_v01_pb_t_kernel(
                     relu(c, 1, 2 * pair + l, h1[:, l, :])
 
         def add_nodes(c):
-            runs = width(c) // RUN
-            first_run = P * FIRST_TILE[c] // RUN
+            rows_i = ROWS_TILE * CHUNK_TILES[c]
+            first_i = ROWS_TILE * FIRST_TILE[c]
             s_lo = work.tile([P, width(c), PACK], BF16, align_bytes=64, bufs=1)
             nc.gpsimd.tensor_tensor(
-                out=s_lo[:].rearrange("p (n i) t -> p n t i", i=RUN),
-                in0=r_of[c, 0][:].rearrange("p t (n i) -> p n t i", i=RUN),
-                in1=x_runs[:].rearrange("p i n t -> p (i n) t")[:, first_run : first_run + runs, :]
-                .unsqueeze(3)
-                .to_broadcast([P, runs, PACK, RUN]),
+                out=s_lo[:].rearrange("p (i j) t -> p i j t", j=NODES),
+                in0=r_of[c, 0][:].rearrange("p t (i j) -> p i j t", j=NODES),
+                in1=x_words[:, first_i : first_i + rows_i, :]
+                .unsqueeze(2)
+                .to_broadcast([P, rows_i, NODES, PACK]),
                 op=ALU.add,
             )
             s_grp_of[c, 0] = s_lo
@@ -462,7 +453,6 @@ def tile_edgeupdaterwrapper_v01_pb_t_kernel(
             group_w2_hi(nc.vector.tensor_copy, plane_t)
         quantise_w2(1)
         fill_node_j(0, 4)
-        fill_node_i(0, 8)
 
         for j in range(N_CHUNKS + 3):
             if live(j):
@@ -498,5 +488,4 @@ def tile_edgeupdaterwrapper_v01_pb_t_kernel(
                 prepare_stage2()
                 fill_node_j(4, 8)
             if j == 1:
-                fill_node_i(8, NODES)
                 fill_node_j(8, ALL_TILES)

@@ -21,7 +21,7 @@ EDGE_F = 256
 MID = 2 * NODE_F + EDGE_F
 EPS = 1e-5
 
-CHUNK_TILES = [2] * 15 + [1] * 2
+CHUNK_TILES = [1] + [2] * 15 + [1]
 N_CHUNKS = len(CHUNK_TILES)
 FIRST_TILE = [sum(CHUNK_TILES[:c]) for c in range(N_CHUNKS)]
 ALL_TILES = EDGES // P
@@ -59,8 +59,7 @@ def tile_edgeupdaterwrapper_v01_pb_t_kernel(
         nc.vector.memset(vec_rows[:], 0.0)
         ones_bf = keep.tile([P, P], BF16)
         nc.vector.memset(ones_bf[:], 1.0)
-        x_words = keep.tile([P, NODES, PACK], BF16)
-        nc.vector.memset(x_words[:], 0.0)
+        x_words = keep.tile([P, NODES, 3], BF16)
 
         hid_sb = keep.tile([P, ALL_TILES, HID], BF16)
         z_mixed = keep.tile([P, ALL_TILES, HID], BF16)
@@ -91,12 +90,12 @@ def tile_edgeupdaterwrapper_v01_pb_t_kernel(
                 )
 
         xd2 = keep.tile([P, NODE_F], BF16)
-        load_hid(0, 2)
         load_w2(0)
+        load_hid(0, 1)
         nc.sync.dma_start(out=xd2[0:NODES, :], in_=xd)
         nc.sync.dma_start(out=xd2[NODES:P, :], in_=xd)
         load_w2(1)
-        load_hid(2, 4)
+        load_hid(1, 4)
         load_p_ln(0, LOAD)
 
         nc.scalar.dma_start(out=b2_rows[0:4, 0:P], in_=b2[0:512].rearrange("(t c) -> t c", t=4))
@@ -136,8 +135,25 @@ def tile_edgeupdaterwrapper_v01_pb_t_kernel(
 
         b2_lo = keep.tile([P, PACK], F32)
         b2_hi = keep.tile([P, PACK], F32)
-        neg_b3 = keep.tile([P, 1], F32)
-        b3_plus_x = keep.tile([P, NODES], F32)
+        last_rows = ROWS_TILE * CHUNK_TILES[-1]
+        x_last = keep.tile([P, last_rows, NODES // RUN, PACK, RUN], BF16)
+
+        def fill_x_last():
+            for i in range(last_rows):
+                nc.vector.tensor_copy(
+                    out=x_last[:, i, :, 0:3, :],
+                    in_=x_words[:, NODES - last_rows + i, 0:3]
+                    .unsqueeze(1)
+                    .unsqueeze(3)
+                    .to_broadcast([P, NODES // RUN, 3, RUN]),
+                )
+            nc.vector.tensor_copy(
+                out=x_last[:, :, :, 3, :],
+                in_=x_words[:, :, 0]
+                .rearrange("p (n i) -> p n i", i=RUN)
+                .unsqueeze(1)
+                .to_broadcast([P, last_rows, NODES // RUN, RUN]),
+            )
 
         def node_tables():
             xt_ps = psum.tile([P, 4, P], BF16, tag="q")
@@ -155,12 +171,6 @@ def tile_edgeupdaterwrapper_v01_pb_t_kernel(
             nc.scalar.copy(
                 out=b2_hi[:].rearrange("p (u h) -> p u h", h=2),
                 in_=b2m_ps[:].bitcast(BF16).rearrange("p u (n h) -> p u n h", h=2)[:, :, 0, :],
-            )
-            nc.vector.tensor_scalar(
-                out=neg_b3[:], in0=b2_lo[:, 3:4], scalar1=-1.0, scalar2=None, op0=ALU.mult
-            )
-            nc.vector.tensor_scalar(
-                out=b3_plus_x[:], in0=xt_ps[:, 0, 0:NODES], scalar1=b2_lo[:, 3:4], scalar2=None, op0=ALU.add
             )
             nc.vector.tensor_copy(
                 out=x_words[:, :, 0:3], in_=xt_ps[:, 0:3, 0:NODES].rearrange("p t n -> p n t")
@@ -217,7 +227,7 @@ def tile_edgeupdaterwrapper_v01_pb_t_kernel(
         r_of = {}
         s_grp_of = {}
         s_mx_of = {}
-        ln_of = {}
+        ln_of = {c: {} for c in range(N_CHUNKS)}
 
         def width(c):
             return P * CHUNK_TILES[c]
@@ -274,81 +284,80 @@ def tile_edgeupdaterwrapper_v01_pb_t_kernel(
             bias = (b2_lo, b2_hi)[a][:, t : t + 1]
             nc.scalar.activation(out=r_of[c, a][:, t, :], in_=h, func=ACT.Relu, bias=bias, scale=1.0)
 
-        def stage1_planes_2_3(c):
-            r_lo = work.tile([P, PACK, width(c)], F32)
-            r_of[c, 0] = r_lo
-            h1 = stage1_pair(c, 2)
-            relu(c, 0, 2, h1[:, 0, :])
-            rows_i = ROWS_TILE * CHUNK_TILES[c]
-            nc.vector.scalar_tensor_tensor(
-                out=r_lo[:, 3, :].rearrange("p (i j) -> p i j", j=NODES),
-                in0=h1[:, 1, :].rearrange("p (i j) -> p i j", j=NODES),
-                scalar=neg_b3[:],
-                in1=b3_plus_x[:].unsqueeze(1).to_broadcast([P, rows_i, NODES]),
-                op0=ALU.max,
-                op1=ALU.add,
-            )
-
-        def stage1_rest(c):
-            h1 = stage1_pair(c, 0)
-            for l in range(2):
-                relu(c, 0, l, h1[:, l, :])
-            r_hi = work.tile([P, PACK, width(c)], F32)
-            r_of[c, 1] = r_hi
+        def stage1(c, a):
+            r = work.tile([P, PACK, width(c)], F32, bufs=4)
+            r_of[c, a] = r
             for pair in range(2):
-                h1 = stage1_pair(c, PACK + 2 * pair)
+                h1 = stage1_pair(c, PACK * a + 2 * pair)
                 for l in range(2):
-                    relu(c, 1, 2 * pair + l, h1[:, l, :])
+                    relu(c, a, 2 * pair + l, h1[:, l, :])
+
+        def new_s(c):
+            s_grp = work.tile([P, 2, width(c), PACK], BF16, align_bytes=64, bufs=1)
+            s_grp_of[c] = s_grp
 
         def add_nodes(c):
             rows_i = ROWS_TILE * CHUNK_TILES[c]
             first_i = ROWS_TILE * FIRST_TILE[c]
-            s_lo = work.tile([P, width(c), PACK], BF16, align_bytes=64, bufs=1)
+            r = r_of[c, 0][:].rearrange("p t (i j) -> p i j t", j=NODES)
+            s = s_grp_of[c][:, 0, :, :].rearrange("p (i j) t -> p i j t", j=NODES)
             nc.gpsimd.tensor_tensor(
-                out=s_lo[:].rearrange("p (i j) t -> p i j t", j=NODES),
-                in0=r_of[c, 0][:].rearrange("p t (i j) -> p i j t", j=NODES),
+                out=s[:, :, :, 0:3],
+                in0=r[:, :, :, 0:3],
                 in1=x_words[:, first_i : first_i + rows_i, :]
                 .unsqueeze(2)
-                .to_broadcast([P, rows_i, NODES, PACK]),
+                .to_broadcast([P, rows_i, NODES, 3]),
                 op=ALU.add,
             )
-            s_grp_of[c, 0] = s_lo
+            nc.gpsimd.tensor_tensor(
+                out=s[:, :, :, 3],
+                in0=r[:, :, :, 3],
+                in1=x_words[:, :, 0].unsqueeze(1).to_broadcast([P, rows_i, NODES]),
+                op=ALU.add,
+            )
+
+        def add_in_runs(s, r, z):
+            nc.vector.tensor_tensor(
+                out=s.rearrange("p (n i) t -> p n t i", i=RUN),
+                in0=r[:].rearrange("p t (n i) -> p n t i", i=RUN),
+                in1=z,
+                op=ALU.add,
+            )
+
+        def add_nodes_last(c):
+            add_in_runs(
+                s_grp_of[c][:, 0, :, :], r_of[c, 0], x_last[:].rearrange("p r n t i -> p (r n) t i")
+            )
 
         def add_z(c):
-            s_hi = work.tile([P, width(c), PACK], BF16, align_bytes=64)
-            nc.vector.tensor_tensor(
-                out=s_hi[:].rearrange("p (n i) t -> p n t i", i=RUN),
-                in0=r_of[c, 1][:].rearrange("p t (n i) -> p n t i", i=RUN),
-                in1=z_words_of[c][:].bitcast(BF16).rearrange("p (n i) t -> p n t i", i=RUN),
-                op=ALU.add,
-            )
-            s_grp_of[c, 1] = s_hi
+            z = z_words_of[c][:].bitcast(BF16).rearrange("p (n i) t -> p n t i", i=RUN)
+            add_in_runs(s_grp_of[c][:, 1, :, :], r_of[c, 1], z)
 
-        def quantise_s(c, a):
-            s_codes = work.tile([P, width(c)], U32, align_bytes=64, bufs=4)
-            s_scales = work.tile([P, width(c)], U8, align_bytes=64, bufs=4)
+        def quantise_s(c):
+            s_codes = work.tile([P, 2, width(c)], U32, align_bytes=64)
+            s_scales = work.tile([P, 2, width(c)], U8, align_bytes=64)
             nc.vector.quantize_mx(
-                out=s_codes[:].bitcast(FP8X4),
-                scales=s_scales[:],
-                in_=s_grp_of[c, a][:].rearrange("p e t -> p (e t)"),
+                out=s_codes[:].rearrange("p a e -> p (a e)").bitcast(FP8X4),
+                scales=s_scales[:].rearrange("p a e -> p (a e)"),
+                in_=s_grp_of[c][:].rearrange("p a e t -> p (a e t)"),
             )
-            s_mx_of[c, a] = (s_codes, s_scales)
+            s_mx_of[c] = (s_codes, s_scales)
 
         def stage2(c):
+            s_codes, s_scales = s_mx_of[c]
             z2 = psum.tile([P, CHUNK_TILES[c], EDGE_F], F32, tag="z2")
             for n in range(CHUNK_TILES[c]):
                 for a in range(2):
-                    s_codes, s_scales = s_mx_of[c, a]
                     nc.tensor.matmul_mx(
                         out=z2[:, n, :],
-                        lhsT=s_codes[:, P * n : P * (n + 1)].bitcast(FP8X4),
-                        lhsT_scale=s_scales[:, P * n : P * (n + 1)],
+                        lhsT=s_codes[:, a, P * n : P * (n + 1)].bitcast(FP8X4),
+                        lhsT_scale=s_scales[:, a, P * n : P * (n + 1)],
                         rhs=wo_codes[:, EDGE_F * a : EDGE_F * (a + 1)].bitcast(FP8X4),
                         rhs_scale=wo_scales[:, EDGE_F * a : EDGE_F * (a + 1)],
                         start=(a == 0),
                         stop=(a == 1),
                     )
-            ln_of[c] = {"z2": z2}
+            ln_of[c]["z2"] = z2
 
         def add_bo(c):
             zb = work.tile([P, CHUNK_TILES[c], EDGE_F], F32, bufs=4)
@@ -388,8 +397,8 @@ def tile_edgeupdaterwrapper_v01_pb_t_kernel(
             ln_of[c]["rstd"] = rstd
             ln_of[c]["neg_mean"] = neg_mean
 
-        def residual(c):
-            q = psum.tile([P, CHUNK_TILES[c], EDGE_F], F32, tag="q")
+        def residual(c, tag="q", bufs=1):
+            q = psum.tile([P, CHUNK_TILES[c], EDGE_F], F32, tag=tag, bufs=bufs)
             for n in range(CHUNK_TILES[c]):
                 nc.tensor.matmul(
                     q[:, n, :].rearrange("p (g f) -> p g f", g=2),
@@ -438,54 +447,79 @@ def tile_edgeupdaterwrapper_v01_pb_t_kernel(
                 in_=result[:],
             )
 
-        def live(c):
-            return 0 <= c < N_CHUNKS
-
         bring_hid(0)
         nc.vector.tensor_copy(out=w2_grp[:, 0:512, :], in_=w2_raw[:, :, 0:512].rearrange("p t f -> p f t"))
-        quantise_hid(0)
         quantise_w2(0)
+        quantise_hid(0)
         node_tables()
-        bring_hid(1)
         for plane_t in (2, 3):
             group_w2_hi(nc.scalar.copy, plane_t)
         for plane_t in (0, 1):
             group_w2_hi(nc.vector.tensor_copy, plane_t)
+        stage1(0, 0)
+        new_s(0)
+        add_nodes(0)
         quantise_w2(1)
+        bring_hid(1)
+        stage1(0, 1)
         fill_node_j(0, 4)
+        quantise_hid(1)
+        bring_z(0)
+        bring_hid(2)
+        stage1(1, 0)
+        add_z(0)
+        prepare_stage2()
+        fill_node_j(4, 8)
 
-        for j in range(N_CHUNKS + 3):
-            if live(j):
-                stage1_planes_2_3(j)
-            if live(j + 1):
-                quantise_hid(j + 1)
-            if live(j - 1):
-                quantise_s(j - 1, 1)
-            if live(j - 3):
+        last = N_CHUNKS - 1
+        for j in range(1, last):
+            quantise_hid(j + 1)
+            if j >= 3:
                 centre_and_gain(j - 3)
-            if live(j - 1):
-                quantise_s(j - 1, 0)
-            if live(j):
-                stage1_rest(j)
-                add_nodes(j)
-            if live(j - 3):
+            quantise_s(j - 1)
+            new_s(j)
+            add_nodes(j)
+            stage1(j, 1)
+            if j >= 3:
                 residual(j - 3)
-            if live(j):
-                bring_z(j)
-            if live(j + 2):
+            bring_z(j)
+            if j + 2 <= last:
                 bring_hid(j + 2)
-            if live(j - 1):
-                stage2(j - 1)
-            if live(j - 2):
+            if j >= 2:
                 statistics(j - 2)
-            if live(j - 3):
+            stage1(j + 1, 0)
+            stage2(j - 1)
+            if j >= 3:
                 finish(j - 3)
-            if live(j - 1):
-                add_bo(j - 1)
-            if live(j):
-                add_z(j)
-            if j == 0:
-                prepare_stage2()
-                fill_node_j(4, 8)
+            add_bo(j - 1)
+            add_z(j)
             if j == 1:
                 fill_node_j(8, ALL_TILES)
+                fill_x_last()
+
+        quantise_s(last - 1)
+        centre_and_gain(last - 3)
+        stage1(last, 1)
+        residual(last - 3)
+        bring_z(last)
+        stage2(last - 1)
+        statistics(last - 2)
+        finish(last - 3)
+        new_s(last)
+        add_nodes_last(last)
+        add_bo(last - 1)
+        add_z(last)
+        quantise_s(last)
+        residual(last - 2)
+        residual(last - 1, tag="hid_t")
+        residual(last, tag="h1", bufs=4)
+        stage2(last)
+        statistics(last - 1)
+        centre_and_gain(last - 2)
+        finish(last - 2)
+        add_bo(last)
+        statistics(last)
+        centre_and_gain(last - 1)
+        finish(last - 1)
+        centre_and_gain(last)
+        finish(last)

@@ -156,11 +156,11 @@ def tile_edgeupdaterwrapper_v01_pb_t_kernel(
             )
 
         def node_tables():
-            xt_ps = psum.tile([P, 4, P], BF16, tag="q")
+            xt_ps = psum.tile([P, 4, P], BF16, tag="ln")
             for t in range(3):
                 nc.tensor.transpose(xt_ps[:, t, :], xd2[:, P * t : P * (t + 1)], ident_bf[:])
             nc.tensor.transpose(xt_ps[:, 3, :], b2_rows[:, 0:P], ident_bf[:])
-            b2m_ps = psum.tile([P, 2, P], F32, tag="z2")
+            b2m_ps = psum.tile([P, 2, P], F32, tag="z_t")
             for u in range(2):
                 nc.tensor.transpose(
                     b2m_ps[:, u, :],
@@ -201,20 +201,20 @@ def tile_edgeupdaterwrapper_v01_pb_t_kernel(
         wo_grp = keep.tile([P, 2, EDGE_F, PACK], BF16, align_bytes=64)
         wo_codes = keep.tile([P, 2 * EDGE_F], U32, align_bytes=64)
         wo_scales = keep.tile([P, 2 * EDGE_F], U8, align_bytes=64)
-        bo_g = keep.tile([P, 2, EDGE_F], F32)
-        bo_bc = bo_g[:, 0, :]
-        g_bc = bo_g[:, 1, :]
+        bo_bc = keep.tile([P, EDGE_F], F32)
+        g_ps = psum.tile([P, EDGE_F], F32, tag="g")
 
         def prepare_stage2():
             for a in range(2):
                 nc.vector.tensor_copy(
                     out=wo_grp[:, a, :, :], in_=wo_raw[:, a, :, :].rearrange("p t f -> p f t")
                 )
-            bc_ps = psum.tile([P, 2 * EDGE_F], F32, tag="q")
+            bo_ps = psum.tile([P, EDGE_F], F32, tag="ln")
+            nc.tensor.matmul(bo_ps[:], lhsT=ones_bf[:], rhs=vec_rows[:, 0:EDGE_F], start=True, stop=True)
             nc.tensor.matmul(
-                bc_ps[:], lhsT=ones_bf[:], rhs=vec_rows[:, 0 : 2 * EDGE_F], start=True, stop=True
+                g_ps[:], lhsT=ones_bf[:], rhs=vec_rows[:, EDGE_F : 2 * EDGE_F], start=True, stop=True
             )
-            nc.vector.tensor_copy(out=bo_g[:].rearrange("p a f -> p (a f)"), in_=bc_ps[:])
+            nc.vector.tensor_copy(out=bo_bc[:], in_=bo_ps[:])
             nc.vector.quantize_mx(
                 out=wo_codes[:].bitcast(FP8X4),
                 scales=wo_scales[:],
@@ -345,7 +345,7 @@ def tile_edgeupdaterwrapper_v01_pb_t_kernel(
 
         def stage2(c):
             s_codes, s_scales = s_mx_of[c]
-            z2 = psum.tile([P, CHUNK_TILES[c], EDGE_F], F32, tag="z2")
+            z2 = psum.tile([P, CHUNK_TILES[c], EDGE_F], F32, tag="ln")
             for n in range(CHUNK_TILES[c]):
                 for a in range(2):
                     nc.tensor.matmul_mx(
@@ -367,7 +367,7 @@ def tile_edgeupdaterwrapper_v01_pb_t_kernel(
                     out=zb[:, n, :],
                     in0=ln_of[c]["z2"][:, n, :],
                     scalar=1.0,
-                    in1=bo_bc,
+                    in1=bo_bc[:],
                     op0=ALU.mult,
                     op1=ALU.add,
                     accum_out=row_sum[:, n : n + 1],
@@ -397,7 +397,7 @@ def tile_edgeupdaterwrapper_v01_pb_t_kernel(
             ln_of[c]["rstd"] = rstd
             ln_of[c]["neg_mean"] = neg_mean
 
-        def residual(c, tag="q", bufs=1):
+        def residual(c, tag="ln", bufs=1):
             q = psum.tile([P, CHUNK_TILES[c], EDGE_F], F32, tag=tag, bufs=bufs)
             for n in range(CHUNK_TILES[c]):
                 nc.tensor.matmul(
@@ -423,7 +423,7 @@ def tile_edgeupdaterwrapper_v01_pb_t_kernel(
                     out=scaled[:, n, :],
                     in0=ln_of[c]["zb"][:, n, :],
                     scalar=ln_of[c]["neg_mean"][:, n : n + 1],
-                    in1=g_bc,
+                    in1=g_ps[:],
                     op0=ALU.add,
                     op1=ALU.mult,
                 )
@@ -474,8 +474,6 @@ def tile_edgeupdaterwrapper_v01_pb_t_kernel(
         last = N_CHUNKS - 1
         for j in range(1, last):
             quantise_hid(j + 1)
-            if j >= 3:
-                centre_and_gain(j - 3)
             quantise_s(j - 1)
             new_s(j)
             add_nodes(j)
@@ -488,31 +486,32 @@ def tile_edgeupdaterwrapper_v01_pb_t_kernel(
             if j >= 2:
                 statistics(j - 2)
             stage1(j + 1, 0)
-            stage2(j - 1)
             if j >= 3:
+                centre_and_gain(j - 3)
                 finish(j - 3)
-            add_bo(j - 1)
+            stage2(j - 1)
             add_z(j)
+            add_bo(j - 1)
             if j == 1:
                 fill_node_j(8, ALL_TILES)
                 fill_x_last()
 
         quantise_s(last - 1)
-        centre_and_gain(last - 3)
         stage1(last, 1)
         residual(last - 3)
         bring_z(last)
-        stage2(last - 1)
         statistics(last - 2)
+        centre_and_gain(last - 3)
         finish(last - 3)
+        stage2(last - 1)
         new_s(last)
         add_nodes_last(last)
-        add_bo(last - 1)
         add_z(last)
         quantise_s(last)
-        residual(last - 2)
-        residual(last - 1, tag="hid_t")
+        residual(last - 2, tag="hid_t")
+        residual(last - 1, tag="h1", bufs=4)
         residual(last, tag="h1", bufs=4)
+        add_bo(last - 1)
         stage2(last)
         statistics(last - 1)
         centre_and_gain(last - 2)

@@ -27,6 +27,7 @@ FIRST_TILE = [sum(CHUNK_TILES[:c]) for c in range(N_CHUNKS)]
 ALL_TILES = EDGES // P
 ROWS_TILE = P // NODES
 RUN = 4
+FILLED = 13
 LOAD = 4
 
 FLOPS = 2 * EDGES * HID * MID + 2 * EDGES * MID * EDGE_F
@@ -59,7 +60,7 @@ def tile_edgeupdaterwrapper_v01_pb_t_kernel(
         nc.vector.memset(vec_rows[:], 0.0)
         ones_bf = keep.tile([P, P], BF16)
         nc.vector.memset(ones_bf[:], 1.0)
-        x_words = keep.tile([P, NODES, 3], BF16)
+        x_words = keep.tile([P, NODES, 3], F32)
 
         hid_sb = keep.tile([P, ALL_TILES, HID], BF16)
         z_mixed = keep.tile([P, ALL_TILES, HID], BF16)
@@ -78,6 +79,14 @@ def tile_edgeupdaterwrapper_v01_pb_t_kernel(
                     in_=p_rows[P * first : P * last, P * g : P * (g + 1)].rearrange("(T p) f -> p T f", p=P),
                 )
 
+        def load_node_j(first, last):
+            for half in range(2):
+                for g in range(2):
+                    nc.sync.dma_start(
+                        out=z_cols[NODES * half : NODES * (half + 1), first:last, g, 0, :],
+                        in_=xd[:, P * (g + 1) : P * (g + 2)].unsqueeze(1).to_broadcast([NODES, last - first, P]),
+                    )
+
         w2_raw = keep.tile([P, PACK, MID], BF16)
 
         def load_w2(a):
@@ -92,19 +101,17 @@ def tile_edgeupdaterwrapper_v01_pb_t_kernel(
         xd2 = keep.tile([P, NODE_F], BF16)
         load_w2(0)
         load_hid(0, 1)
+        load_w2(1)
+        nc.scalar.dma_start(out=b2_rows[0:4, 0:P], in_=b2[0:512].rearrange("(t c) -> t c", t=4))
+        nc.scalar.dma_start(
+            out=b2_rows[0:1, P : P + HID].rearrange("o (g k c) -> o g k c", g=2, k=2),
+            in_=b2[512:1024].rearrange("(o k g c) -> o g k c", o=1, g=2, k=2),
+        )
         nc.sync.dma_start(out=xd2[0:NODES, :], in_=xd)
         nc.sync.dma_start(out=xd2[NODES:P, :], in_=xd)
-        load_w2(1)
-        load_hid(1, 4)
-        load_p_ln(0, LOAD)
+        load_hid(1, 1 + LOAD)
+        load_p_ln(0, 1 + LOAD)
 
-        nc.scalar.dma_start(out=b2_rows[0:4, 0:P], in_=b2[0:512].rearrange("(t c) -> t c", t=4))
-        b2_mixed = b2_rows[0:1, P : P + HID].rearrange("o (g k c) -> o g k c", g=2, k=2)
-        for k in range(2):
-            nc.scalar.dma_start(
-                out=b2_mixed[:, :, k, :],
-                in_=b2[512 + 256 * k : 768 + 256 * k].rearrange("(o g c) -> o g c", o=1, g=2),
-            )
         for n, vec in enumerate((bo, ln_out_g, ln_out_b)):
             nc.gpsimd.dma_start(
                 out=vec_rows[0:1, EDGE_F * n : EDGE_F * (n + 1)],
@@ -122,9 +129,12 @@ def tile_edgeupdaterwrapper_v01_pb_t_kernel(
                 out=wo_raw[64 * k : 64 * k + 64, 1, :, :].rearrange("m (u h) f -> m u (h f)", h=2),
                 in_=Wo[512 + 256 * k : 768 + 256 * k, :].rearrange("(u m h) f -> m u (h f)", u=2, h=2),
             )
-        for first in range(LOAD, ALL_TILES, LOAD):
-            load_hid(first, first + LOAD)
-            load_p_ln(first, first + LOAD)
+        for first in range(1 + LOAD, ALL_TILES, LOAD):
+            after = min(first + LOAD, ALL_TILES)
+            load_hid(first, after)
+            load_p_ln(first, after)
+            if first >= FILLED:
+                load_node_j(first, after)
 
         def fill_node_j(first, last):
             for g in range(2):
@@ -156,7 +166,7 @@ def tile_edgeupdaterwrapper_v01_pb_t_kernel(
             )
 
         def node_tables():
-            xt_ps = psum.tile([P, 4, P], BF16, tag="ln")
+            xt_ps = psum.tile([P, 4, P], BF16, tag="q")
             for t in range(3):
                 nc.tensor.transpose(xt_ps[:, t, :], xd2[:, P * t : P * (t + 1)], ident_bf[:])
             nc.tensor.transpose(xt_ps[:, 3, :], b2_rows[:, 0:P], ident_bf[:])
@@ -204,17 +214,22 @@ def tile_edgeupdaterwrapper_v01_pb_t_kernel(
         bo_bc = keep.tile([P, EDGE_F], F32)
         g_ps = psum.tile([P, EDGE_F], F32, tag="g")
 
-        def prepare_stage2():
-            for a in range(2):
-                nc.vector.tensor_copy(
-                    out=wo_grp[:, a, :, :], in_=wo_raw[:, a, :, :].rearrange("p t f -> p f t")
-                )
-            bo_ps = psum.tile([P, EDGE_F], F32, tag="ln")
+        def broadcast_bo_g():
+            bo_ps = psum.tile([P, EDGE_F], F32, tag="z2")
             nc.tensor.matmul(bo_ps[:], lhsT=ones_bf[:], rhs=vec_rows[:, 0:EDGE_F], start=True, stop=True)
             nc.tensor.matmul(
                 g_ps[:], lhsT=ones_bf[:], rhs=vec_rows[:, EDGE_F : 2 * EDGE_F], start=True, stop=True
             )
             nc.vector.tensor_copy(out=bo_bc[:], in_=bo_ps[:])
+
+        def group_wo():
+            for a in range(2):
+                nc.vector.tensor_copy(
+                    out=wo_grp[:, a, :, :].rearrange("p (n i) t -> p n t i", i=RUN),
+                    in_=wo_raw[:, a, :, :].rearrange("p t (n i) -> p n t i", i=RUN),
+                )
+
+        def quantise_wo():
             nc.vector.quantize_mx(
                 out=wo_codes[:].bitcast(FP8X4),
                 scales=wo_scales[:],
@@ -266,7 +281,7 @@ def tile_edgeupdaterwrapper_v01_pb_t_kernel(
 
         def stage1_pair(c, first_plane):
             hid_codes, hid_scales = hid_mx_of[c]
-            h1 = psum.tile([P, 2, width(c)], F32, tag="h1", bufs=4)
+            h1 = psum.tile([P, 2, width(c)], F32, tag="h1", bufs=3)
             for l in range(2):
                 plane = first_plane + l
                 nc.tensor.matmul_mx(
@@ -345,7 +360,7 @@ def tile_edgeupdaterwrapper_v01_pb_t_kernel(
 
         def stage2(c):
             s_codes, s_scales = s_mx_of[c]
-            z2 = psum.tile([P, CHUNK_TILES[c], EDGE_F], F32, tag="ln")
+            z2 = psum.tile([P, CHUNK_TILES[c], EDGE_F], F32, tag="z2")
             for n in range(CHUNK_TILES[c]):
                 for a in range(2):
                     nc.tensor.matmul_mx(
@@ -397,7 +412,7 @@ def tile_edgeupdaterwrapper_v01_pb_t_kernel(
             ln_of[c]["rstd"] = rstd
             ln_of[c]["neg_mean"] = neg_mean
 
-        def residual(c, tag="ln", bufs=1):
+        def residual(c, tag="q", bufs=1):
             q = psum.tile([P, CHUNK_TILES[c], EDGE_F], F32, tag=tag, bufs=bufs)
             for n in range(CHUNK_TILES[c]):
                 nc.tensor.matmul(
@@ -448,28 +463,32 @@ def tile_edgeupdaterwrapper_v01_pb_t_kernel(
             )
 
         bring_hid(0)
-        nc.vector.tensor_copy(out=w2_grp[:, 0:512, :], in_=w2_raw[:, :, 0:512].rearrange("p t f -> p f t"))
+        nc.vector.tensor_copy(
+            out=w2_grp[:, 0:512, :].rearrange("p (n i) t -> p n t i", i=RUN),
+            in_=w2_raw[:, :, 0:512].rearrange("p t (n i) -> p n t i", i=RUN),
+        )
+        group_w2_hi(nc.vector.tensor_copy, 0)
         quantise_w2(0)
         quantise_hid(0)
-        node_tables()
         for plane_t in (2, 3):
             group_w2_hi(nc.scalar.copy, plane_t)
-        for plane_t in (0, 1):
-            group_w2_hi(nc.vector.tensor_copy, plane_t)
+        group_w2_hi(nc.vector.tensor_copy, 1)
+        node_tables()
         stage1(0, 0)
         new_s(0)
-        add_nodes(0)
         quantise_w2(1)
+        fill_node_j(0, FILLED)
+        add_nodes(0)
+        broadcast_bo_g()
         bring_hid(1)
         stage1(0, 1)
-        fill_node_j(0, 4)
-        quantise_hid(1)
         bring_z(0)
-        bring_hid(2)
+        quantise_hid(1)
+        group_wo()
         stage1(1, 0)
+        bring_hid(2)
         add_z(0)
-        prepare_stage2()
-        fill_node_j(4, 8)
+        quantise_wo()
 
         last = N_CHUNKS - 1
         for j in range(1, last):
@@ -480,41 +499,40 @@ def tile_edgeupdaterwrapper_v01_pb_t_kernel(
             stage1(j, 1)
             if j >= 3:
                 residual(j - 3)
+            if j >= 2:
+                statistics(j - 2)
             bring_z(j)
             if j + 2 <= last:
                 bring_hid(j + 2)
-            if j >= 2:
-                statistics(j - 2)
             stage1(j + 1, 0)
-            if j >= 3:
-                centre_and_gain(j - 3)
-                finish(j - 3)
             stage2(j - 1)
+            if j >= 3:
+                finish(j - 3)
             add_z(j)
+            if j >= 2:
+                centre_and_gain(j - 2)
             add_bo(j - 1)
             if j == 1:
-                fill_node_j(8, ALL_TILES)
                 fill_x_last()
 
         quantise_s(last - 1)
         stage1(last, 1)
         residual(last - 3)
-        bring_z(last)
         statistics(last - 2)
-        centre_and_gain(last - 3)
-        finish(last - 3)
+        bring_z(last)
         stage2(last - 1)
         new_s(last)
+        finish(last - 3)
         add_nodes_last(last)
         add_z(last)
+        centre_and_gain(last - 2)
         quantise_s(last)
-        residual(last - 2, tag="hid_t")
-        residual(last - 1, tag="h1", bufs=4)
-        residual(last, tag="h1", bufs=4)
+        residual(last - 2)
+        residual(last - 1, tag="hid_t")
+        residual(last, tag="h1", bufs=3)
         add_bo(last - 1)
         stage2(last)
         statistics(last - 1)
-        centre_and_gain(last - 2)
         finish(last - 2)
         add_bo(last)
         statistics(last)

@@ -27,7 +27,6 @@ FIRST_TILE = [sum(CHUNK_TILES[:c]) for c in range(N_CHUNKS)]
 ALL_TILES = EDGES // P
 ROWS_TILE = P // NODES
 RUN = 4
-FILLED = 13
 LOAD = 4
 
 FLOPS = 2 * EDGES * HID * MID + 2 * EDGES * MID * EDGE_F
@@ -60,7 +59,8 @@ def tile_edgeupdaterwrapper_v01_pb_t_kernel(
         nc.vector.memset(vec_rows[:], 0.0)
         ones_bf = keep.tile([P, P], BF16)
         nc.vector.memset(ones_bf[:], 1.0)
-        x_words = keep.tile([P, NODES, 3], F32)
+        x_words = keep.tile([P, NODES, PACK], BF16)
+        nc.vector.memset(x_words[:], 0.0)
 
         hid_sb = keep.tile([P, ALL_TILES, HID], BF16)
         z_mixed = keep.tile([P, ALL_TILES, HID], BF16)
@@ -78,14 +78,6 @@ def tile_edgeupdaterwrapper_v01_pb_t_kernel(
                     out=z_cols[:, first:last, g, 1, :],
                     in_=p_rows[P * first : P * last, P * g : P * (g + 1)].rearrange("(T p) f -> p T f", p=P),
                 )
-
-        def load_node_j(first, last):
-            for half in range(2):
-                for g in range(2):
-                    nc.sync.dma_start(
-                        out=z_cols[NODES * half : NODES * (half + 1), first:last, g, 0, :],
-                        in_=xd[:, P * (g + 1) : P * (g + 2)].unsqueeze(1).to_broadcast([NODES, last - first, P]),
-                    )
 
         w2_raw = keep.tile([P, PACK, MID], BF16)
 
@@ -133,8 +125,6 @@ def tile_edgeupdaterwrapper_v01_pb_t_kernel(
             after = min(first + LOAD, ALL_TILES)
             load_hid(first, after)
             load_p_ln(first, after)
-            if first >= FILLED:
-                load_node_j(first, after)
 
         def fill_node_j(first, last):
             for g in range(2):
@@ -145,26 +135,8 @@ def tile_edgeupdaterwrapper_v01_pb_t_kernel(
 
         b2_lo = keep.tile([P, PACK], F32)
         b2_hi = keep.tile([P, PACK], F32)
-        last_rows = ROWS_TILE * CHUNK_TILES[-1]
-        x_last = keep.tile([P, last_rows, NODES // RUN, PACK, RUN], BF16)
-
-        def fill_x_last():
-            for i in range(last_rows):
-                nc.vector.tensor_copy(
-                    out=x_last[:, i, :, 0:3, :],
-                    in_=x_words[:, NODES - last_rows + i, 0:3]
-                    .unsqueeze(1)
-                    .unsqueeze(3)
-                    .to_broadcast([P, NODES // RUN, 3, RUN]),
-                )
-            nc.vector.tensor_copy(
-                out=x_last[:, :, :, 3, :],
-                in_=x_words[:, :, 0]
-                .rearrange("p (n i) -> p n i", i=RUN)
-                .unsqueeze(1)
-                .to_broadcast([P, last_rows, NODES // RUN, RUN]),
-            )
-
+        neg_b3 = keep.tile([P, 1], F32)
+        b3_plus_x = keep.tile([P, NODES], F32)
         def node_tables():
             xt_ps = psum.tile([P, 4, P], BF16, tag="q")
             for t in range(3):
@@ -181,6 +153,12 @@ def tile_edgeupdaterwrapper_v01_pb_t_kernel(
             nc.scalar.copy(
                 out=b2_hi[:].rearrange("p (u h) -> p u h", h=2),
                 in_=b2m_ps[:].bitcast(BF16).rearrange("p u (n h) -> p u n h", h=2)[:, :, 0, :],
+            )
+            nc.vector.tensor_scalar(
+                out=neg_b3[:], in0=b2_lo[:, 3:4], scalar1=-1.0, scalar2=None, op0=ALU.mult
+            )
+            nc.vector.tensor_scalar(
+                out=b3_plus_x[:], in0=xt_ps[:, 0, 0:NODES], scalar1=b2_lo[:, 3:4], scalar2=None, op0=ALU.add
             )
             nc.vector.tensor_copy(
                 out=x_words[:, :, 0:3], in_=xt_ps[:, 0:3, 0:NODES].rearrange("p t n -> p n t")
@@ -240,6 +218,7 @@ def tile_edgeupdaterwrapper_v01_pb_t_kernel(
         z_words_of = {}
         hid_mx_of = {}
         r_of = {}
+        plane3_of = {}
         s_grp_of = {}
         s_mx_of = {}
         ln_of = {c: {} for c in range(N_CHUNKS)}
@@ -305,7 +284,21 @@ def tile_edgeupdaterwrapper_v01_pb_t_kernel(
             for pair in range(2):
                 h1 = stage1_pair(c, PACK * a + 2 * pair)
                 for l in range(2):
+                    if (a, pair, l) == (0, 1, 1):
+                        plane3_of[c] = h1[:, 1, :]
+                        continue
                     relu(c, a, 2 * pair + l, h1[:, l, :])
+
+        def plane3(c):
+            rows_i = ROWS_TILE * CHUNK_TILES[c]
+            nc.vector.scalar_tensor_tensor(
+                out=r_of[c, 0][:, 3, :].rearrange("p (i j) -> p i j", j=NODES),
+                in0=plane3_of[c].rearrange("p (i j) -> p i j", j=NODES),
+                scalar=neg_b3[:],
+                in1=b3_plus_x[:].unsqueeze(1).to_broadcast([P, rows_i, NODES]),
+                op0=ALU.max,
+                op1=ALU.add,
+            )
 
         def new_s(c):
             s_grp = work.tile([P, 2, width(c), PACK], BF16, align_bytes=64, bufs=1)
@@ -314,20 +307,12 @@ def tile_edgeupdaterwrapper_v01_pb_t_kernel(
         def add_nodes(c):
             rows_i = ROWS_TILE * CHUNK_TILES[c]
             first_i = ROWS_TILE * FIRST_TILE[c]
-            r = r_of[c, 0][:].rearrange("p t (i j) -> p i j t", j=NODES)
-            s = s_grp_of[c][:, 0, :, :].rearrange("p (i j) t -> p i j t", j=NODES)
             nc.gpsimd.tensor_tensor(
-                out=s[:, :, :, 0:3],
-                in0=r[:, :, :, 0:3],
+                out=s_grp_of[c][:, 0, :, :].rearrange("p (i j) t -> p i j t", j=NODES),
+                in0=r_of[c, 0][:].rearrange("p t (i j) -> p i j t", j=NODES),
                 in1=x_words[:, first_i : first_i + rows_i, :]
                 .unsqueeze(2)
-                .to_broadcast([P, rows_i, NODES, 3]),
-                op=ALU.add,
-            )
-            nc.gpsimd.tensor_tensor(
-                out=s[:, :, :, 3],
-                in0=r[:, :, :, 3],
-                in1=x_words[:, :, 0].unsqueeze(1).to_broadcast([P, rows_i, NODES]),
+                .to_broadcast([P, rows_i, NODES, PACK]),
                 op=ALU.add,
             )
 
@@ -337,11 +322,6 @@ def tile_edgeupdaterwrapper_v01_pb_t_kernel(
                 in0=r[:].rearrange("p t (n i) -> p n t i", i=RUN),
                 in1=z,
                 op=ALU.add,
-            )
-
-        def add_nodes_last(c):
-            add_in_runs(
-                s_grp_of[c][:, 0, :, :], r_of[c, 0], x_last[:].rearrange("p r n t i -> p (r n) t i")
             )
 
         def add_z(c):
@@ -475,9 +455,10 @@ def tile_edgeupdaterwrapper_v01_pb_t_kernel(
         group_w2_hi(nc.vector.tensor_copy, 1)
         node_tables()
         stage1(0, 0)
+        plane3(0)
         new_s(0)
         quantise_w2(1)
-        fill_node_j(0, FILLED)
+        fill_node_j(0, 5)
         add_nodes(0)
         broadcast_bo_g()
         bring_hid(1)
@@ -488,6 +469,7 @@ def tile_edgeupdaterwrapper_v01_pb_t_kernel(
         stage1(1, 0)
         bring_hid(2)
         add_z(0)
+        plane3(1)
         quantise_wo()
 
         last = N_CHUNKS - 1
@@ -512,8 +494,9 @@ def tile_edgeupdaterwrapper_v01_pb_t_kernel(
             if j >= 2:
                 centre_and_gain(j - 2)
             add_bo(j - 1)
-            if j == 1:
-                fill_x_last()
+            plane3(j + 1)
+            if j in (1, 2, 3):
+                fill_node_j(9 * j - 4, 9 * j + 5)
 
         quantise_s(last - 1)
         stage1(last, 1)
@@ -523,7 +506,7 @@ def tile_edgeupdaterwrapper_v01_pb_t_kernel(
         stage2(last - 1)
         new_s(last)
         finish(last - 3)
-        add_nodes_last(last)
+        add_nodes(last)
         add_z(last)
         centre_and_gain(last - 2)
         quantise_s(last)

@@ -27,6 +27,7 @@ FIRST_TILE = [sum(CHUNK_TILES[:c]) for c in range(N_CHUNKS)]
 ALL_TILES = EDGES // P
 ROWS_TILE = P // NODES
 RUN = 4
+FILLED = 21
 LOAD = 4
 
 FLOPS = 2 * EDGES * HID * MID + 2 * EDGES * MID * EDGE_F
@@ -79,6 +80,14 @@ def tile_edgeupdaterwrapper_v01_pb_t_kernel(
                     in_=p_rows[P * first : P * last, P * g : P * (g + 1)].rearrange("(T p) f -> p T f", p=P),
                 )
 
+        def load_node_j(first, last):
+            for half in range(2):
+                for g in range(2):
+                    nc.sync.dma_start(
+                        out=z_cols[NODES * half : NODES * (half + 1), first:last, g, 0, :],
+                        in_=xd[:, P * (g + 1) : P * (g + 2)].unsqueeze(1).to_broadcast([NODES, last - first, P]),
+                    )
+
         w2_raw = keep.tile([P, PACK, MID], BF16)
 
         def load_w2(a):
@@ -125,6 +134,7 @@ def tile_edgeupdaterwrapper_v01_pb_t_kernel(
             after = min(first + LOAD, ALL_TILES)
             load_hid(first, after)
             load_p_ln(first, after)
+        load_node_j(FILLED, ALL_TILES)
 
         def fill_node_j(first, last):
             for g in range(2):
@@ -474,8 +484,8 @@ def tile_edgeupdaterwrapper_v01_pb_t_kernel(
 
         last = N_CHUNKS - 1
         for j in range(1, last):
-            quantise_hid(j + 1)
             quantise_s(j - 1)
+            quantise_hid(j + 1)
             new_s(j)
             add_nodes(j)
             stage1(j, 1)
@@ -495,8 +505,8 @@ def tile_edgeupdaterwrapper_v01_pb_t_kernel(
                 centre_and_gain(j - 2)
             add_bo(j - 1)
             plane3(j + 1)
-            if j in (1, 2, 3):
-                fill_node_j(9 * j - 4, 9 * j + 5)
+            if j in (1, 2):
+                fill_node_j(8 * j - 3, 8 * j + 5)
 
         quantise_s(last - 1)
         stage1(last, 1)

@@ -28,6 +28,7 @@ ALL_TILES = EDGES // P
 ROWS_TILE = P // NODES
 RUN = 4
 FILLED = 21
+PAIR = 2
 LOAD = 4
 
 FLOPS = 2 * EDGES * HID * MID + 2 * EDGES * MID * EDGE_F
@@ -208,7 +209,7 @@ def tile_edgeupdaterwrapper_v01_pb_t_kernel(
             nc.tensor.matmul(
                 g_ps[:], lhsT=ones_bf[:], rhs=vec_rows[:, EDGE_F : 2 * EDGE_F], start=True, stop=True
             )
-            nc.vector.tensor_copy(out=bo_bc[:], in_=bo_ps[:])
+            nc.scalar.copy(out=bo_bc[:], in_=bo_ps[:])
 
         def group_wo():
             for a in range(2):
@@ -315,16 +316,18 @@ def tile_edgeupdaterwrapper_v01_pb_t_kernel(
             s_grp_of[c] = s_grp
 
         def add_nodes(c):
-            rows_i = ROWS_TILE * CHUNK_TILES[c]
             first_i = ROWS_TILE * FIRST_TILE[c]
-            nc.gpsimd.tensor_tensor(
-                out=s_grp_of[c][:, 0, :, :].rearrange("p (i j) t -> p i j t", j=NODES),
-                in0=r_of[c, 0][:].rearrange("p t (i j) -> p i j t", j=NODES),
-                in1=x_words[:, first_i : first_i + rows_i, :]
-                .unsqueeze(2)
-                .to_broadcast([P, rows_i, NODES, PACK]),
-                op=ALU.add,
-            )
+            for i in range(ROWS_TILE * CHUNK_TILES[c]):
+                edges = slice(NODES * i, NODES * (i + 1))
+                nc.gpsimd.tensor_tensor(
+                    out=s_grp_of[c][:, 0, edges, :].rearrange("p (n k) t -> p n t k", k=PAIR),
+                    in0=r_of[c, 0][:, :, edges].rearrange("p t (n k) -> p n t k", k=PAIR),
+                    in1=x_words[:, first_i + i, :]
+                    .unsqueeze(1)
+                    .unsqueeze(3)
+                    .to_broadcast([P, NODES // PAIR, PACK, PAIR]),
+                    op=ALU.add,
+                )
 
         def add_in_runs(s, r, z):
             nc.vector.tensor_tensor(

from contextlib import ExitStack

import concourse.mybir as mybir
from concourse.masks import make_identity

F32 = mybir.dt.float32
BF16 = mybir.dt.bfloat16
U32 = mybir.dt.uint32
U8 = mybir.dt.uint8
FP8X4 = mybir.dt.float8_e4m3fn_x4
ALU = mybir.AluOpType
ACT = mybir.ActivationFunctionType

P = 128
PACK = 4
NODES = 64
EDGES = NODES * NODES
HID = 512
NODE_F = 384
EDGE_F = 256
MID = 2 * NODE_F + EDGE_F
EPS = 1e-5

CHUNK_TILES = [1] + [2] * 15 + [1]
N_CHUNKS = len(CHUNK_TILES)
FIRST_TILE = [sum(CHUNK_TILES[:c]) for c in range(N_CHUNKS)]
ALL_TILES = EDGES // P
ROWS_TILE = P // NODES
RUN = 4
FILLED = 21
PAIR = 2
LOAD = 4

FLOPS = 2 * EDGES * HID * MID + 2 * EDGES * MID * EDGE_F


def tile_edgeupdaterwrapper_v01_pb_t_kernel(
    tc, hid, x_down, p_ln, W2, b2, Wo, bo, ln_out_g, ln_out_b, out
):
    nc = tc.nc
    hid_rows = hid.flatten_outer_dims()
    p_rows = p_ln.flatten_outer_dims()
    out_rows = out.flatten_outer_dims()
    xd = x_down.flatten_outer_dims()

    with ExitStack() as ctx:
        keep = ctx.enter_context(tc.tile_pool(name="keep", bufs=1))
        work = ctx.enter_context(tc.tile_pool(name="work", bufs=2))
        psum = ctx.enter_context(tc.psum_pool(name="psum", bufs=1))

        ident_f32 = keep.tile([P, P], F32)
        make_identity(nc, ident_f32[:])
        ident_bf = keep.tile([P, P], BF16)
        make_identity(nc, ident_bf[:])
        ctx.enter_context(tc.manual_schedule())
        b2_rows = keep.tile([P, P + HID], BF16)
        nc.vector.memset(b2_rows[:], 0.0)
        eps_col = keep.tile([P, 1], F32)
        nc.vector.memset(eps_col[:], EPS)
        vec_rows = keep.tile([P, 3 * EDGE_F], BF16)
        nc.vector.memset(vec_rows[:], 0.0)
        ones_bf = keep.tile([P, P], BF16)
        nc.vector.memset(ones_bf[:], 1.0)
        x_words = keep.tile([P, NODES, PACK], BF16)
        nc.vector.memset(x_words[:], 0.0)

        hid_sb = keep.tile([P, ALL_TILES, HID], BF16)
        z_mixed = keep.tile([P, ALL_TILES, HID], BF16)
        z_cols = z_mixed[:].rearrange("p T (g k c) -> p T g k c", g=2, k=2)

        def load_hid(first, last):
            nc.sync.dma_start(
                out=hid_sb[:, first:last, :],
                in_=hid_rows[P * first : P * last, :].rearrange("(T p) k -> p T k", p=P),
            )

        def load_p_ln(first, last):
            for g in range(2):
                nc.sync.dma_start(
                    out=z_cols[:, first:last, g, 1, :],
                    in_=p_rows[P * first : P * last, P * g : P * (g + 1)].rearrange("(T p) f -> p T f", p=P),
                )

        def load_node_j(first, last):
            for half in range(2):
                for g in range(2):
                    nc.sync.dma_start(
                        out=z_cols[NODES * half : NODES * (half + 1), first:last, g, 0, :],
                        in_=xd[:, P * (g + 1) : P * (g + 2)].unsqueeze(1).to_broadcast([NODES, last - first, P]),
                    )

        w2_raw = keep.tile([P, PACK, MID], BF16)

        def load_w2(a):
            for u in range(2):
                nc.sync.dma_start(
                    out=w2_raw[:, 2 * u : 2 * u + 2, 512 * a : 512 * (a + 1)],
                    in_=W2[256 * u : 256 * u + 256, 512 * a : 512 * (a + 1)].rearrange(
                        "(p h) f -> p h f", h=2
                    ),
                )

        xd2 = keep.tile([P, NODE_F], BF16)
        load_w2(0)
        load_hid(0, 1)
        load_w2(1)
        nc.scalar.dma_start(out=b2_rows[0:4, 0:P], in_=b2[0:512].rearrange("(t c) -> t c", t=4))
        nc.scalar.dma_start(
            out=b2_rows[0:1, P : P + HID].rearrange("o (g k c) -> o g k c", g=2, k=2),
            in_=b2[512:1024].rearrange("(o k g c) -> o g k c", o=1, g=2, k=2),
        )
        nc.sync.dma_start(out=xd2[0:NODES, :], in_=xd)
        nc.sync.dma_start(out=xd2[NODES:P, :], in_=xd)
        load_hid(1, 1 + LOAD)
        load_p_ln(0, 1 + LOAD)

        for n, vec in enumerate((bo, ln_out_g, ln_out_b)):
            nc.gpsimd.dma_start(
                out=vec_rows[0:1, EDGE_F * n : EDGE_F * (n + 1)],
                in_=vec.rearrange("(o f) -> o f", o=1),
            )
        warm = keep.tile([P, 1], F32)
        nc.scalar.activation(
            out=warm[:], in_=eps_col[:], func=ACT.Abs_reciprocal_sqrt, bias=0.0, scale=1.0
        )

        wo_raw = keep.tile([P, 2, PACK, EDGE_F], BF16)
        nc.sync.dma_start(out=wo_raw[:, 0, :, :], in_=Wo[0:512, :].rearrange("(t p) f -> p t f", p=P))
        for k in range(2):
            nc.sync.dma_start(
                out=wo_raw[64 * k : 64 * k + 64, 1, :, :].rearrange("m (u h) f -> m u (h f)", h=2),
                in_=Wo[512 + 256 * k : 768 + 256 * k, :].rearrange("(u m h) f -> m u (h f)", u=2, h=2),
            )
        for first in range(1 + LOAD, ALL_TILES, LOAD):
            after = min(first + LOAD, ALL_TILES)
            load_hid(first, after)
            load_p_ln(first, after)
        load_node_j(FILLED, ALL_TILES)

        def fill_node_j(first, last):
            for g in range(2):
                nc.vector.tensor_copy(
                    out=z_cols[:, first:last, g, 0, :],
                    in_=xd2[:, P * (g + 1) : P * (g + 2)].unsqueeze(1).to_broadcast([P, last - first, P]),
                )

        b2_lo = keep.tile([P, PACK], F32)
        b2_hi = keep.tile([P, PACK], F32)
        neg_b3 = keep.tile([P, 1], F32)
        b3_plus_x = keep.tile([P, NODES], F32)
        def node_tables():
            xt_ps = psum.tile([P, 4, P], BF16, tag="q")
            for t in range(3):
                nc.tensor.transpose(xt_ps[:, t, :], xd2[:, P * t : P * (t + 1)], ident_bf[:])
            nc.tensor.transpose(xt_ps[:, 3, :], b2_rows[:, 0:P], ident_bf[:])
            b2m_ps = psum.tile([P, 2, P], F32, tag="z_t")
            for u in range(2):
                nc.tensor.transpose(
                    b2m_ps[:, u, :],
                    b2_rows[:, P : P + HID].bitcast(F32)[:, P * u : P * (u + 1)],
                    ident_f32[:],
                )
            nc.scalar.copy(out=b2_lo[:], in_=xt_ps[:, 3, 0:4])
            nc.scalar.copy(
                out=b2_hi[:].rearrange("p (u h) -> p u h", h=2),
                in_=b2m_ps[:].bitcast(BF16).rearrange("p u (n h) -> p u n h", h=2)[:, :, 0, :],
            )
            nc.vector.tensor_scalar(
                out=neg_b3[:], in0=b2_lo[:, 3:4], scalar1=-1.0, scalar2=None, op0=ALU.mult
            )
            nc.vector.tensor_scalar(
                out=b3_plus_x[:], in0=xt_ps[:, 0, 0:NODES], scalar1=b2_lo[:, 3:4], scalar2=None, op0=ALU.add
            )
            nc.vector.tensor_copy(
                out=x_words[:, :, 0:3], in_=xt_ps[:, 0:3, 0:NODES].rearrange("p t n -> p n t")
            )

        w2_grp = keep.tile([P, MID, PACK], BF16, align_bytes=64)
        w2_codes = keep.tile([P, MID], U32, align_bytes=64)
        w2_scales = keep.tile([P, MID], U8, align_bytes=64)
        w2_hi = w2_raw[:, :, 512:1024].rearrange(
            "p t (k u m h) -> p u h k m t", k=2, u=2, m=64, h=2
        )

        def quantise_w2(a):
            nc.vector.quantize_mx(
                out=w2_codes[:, 512 * a : 512 * (a + 1)].bitcast(FP8X4),
                scales=w2_scales[:, 512 * a : 512 * (a + 1)],
                in_=w2_grp[:, 512 * a : 512 * (a + 1), :].rearrange("p f t -> p (f t)"),
            )

        def group_w2_hi(engine_copy, plane_t):
            u, h = plane_t // 2, plane_t % 2
            plane = 4 + plane_t
            engine_copy(
                out=w2_grp[:, P * plane : P * (plane + 1), :].rearrange("p (k m) t -> p k m t", k=2),
                in_=w2_hi[:, u, h],
            )

        wo_grp = keep.tile([P, 2, EDGE_F, PACK], BF16, align_bytes=64)
        wo_codes = keep.tile([P, 2 * EDGE_F], U32, align_bytes=64)
        wo_scales = keep.tile([P, 2 * EDGE_F], U8, align_bytes=64)
        bo_bc = keep.tile([P, EDGE_F], F32)
        g_ps = psum.tile([P, EDGE_F], F32, tag="g")

        def broadcast_bo_g():
            bo_ps = psum.tile([P, EDGE_F], F32, tag="z2")
            nc.tensor.matmul(bo_ps[:], lhsT=ones_bf[:], rhs=vec_rows[:, 0:EDGE_F], start=True, stop=True)
            nc.tensor.matmul(
                g_ps[:], lhsT=ones_bf[:], rhs=vec_rows[:, EDGE_F : 2 * EDGE_F], start=True, stop=True
            )
            nc.scalar.copy(out=bo_bc[:], in_=bo_ps[:])

        def group_wo():
            for a in range(2):
                nc.vector.tensor_copy(
                    out=wo_grp[:, a, :, :].rearrange("p (n i) t -> p n t i", i=RUN),
                    in_=wo_raw[:, a, :, :].rearrange("p t (n i) -> p n t i", i=RUN),
                )

        def quantise_wo():
            nc.vector.quantize_mx(
                out=wo_codes[:].bitcast(FP8X4),
                scales=wo_scales[:],
                in_=wo_grp[:].rearrange("p a f t -> p (a f t)"),
            )

        hid_grp_of = {}
        z_words_of = {}
        hid_mx_of = {}
        r_of = {}
        plane3_of = {}
        s_grp_of = {}
        s_mx_of = {}
        ln_of = {c: {} for c in range(N_CHUNKS)}

        def width(c):
            return P * CHUNK_TILES[c]

        def transpose_words(rows, c, words_t):
            for u in range(2):
                for l in range(CHUNK_TILES[c]):
                    nc.tensor.transpose(
                        words_t[u][:, P * l : P * (l + 1)],
                        rows[:, FIRST_TILE[c] + l, :].bitcast(F32)[:, P * u : P * (u + 1)],
                        ident_f32[:],
                    )

        def bring_hid(c):
            words_t = psum.tile([P, 2, width(c)], F32, tag="hid_t")
            transpose_words(hid_sb, c, [words_t[:, u, :] for u in range(2)])
            hid_grp = work.tile([P, width(c) * PACK], BF16, align_bytes=64, bufs=3)
            nc.scalar.copy(
                out=hid_grp[:].bitcast(F32).rearrange("p (e u) -> p e u", u=2),
                in_=words_t[:].rearrange("p u e -> p e u"),
            )
            hid_grp_of[c] = hid_grp

        def bring_z(c):
            words_t = psum.tile([P, width(c), 2], F32, tag="z_t")
            transpose_words(z_mixed, c, [words_t[:, :, u] for u in range(2)])
            z_words_of[c] = words_t

        def quantise_hid(c):
            hid_codes = work.tile([P, width(c)], U32, align_bytes=64)
            hid_scales = work.tile([P, width(c)], U8, align_bytes=64)
            nc.vector.quantize_mx(
                out=hid_codes[:].bitcast(FP8X4), scales=hid_scales[:], in_=hid_grp_of[c][:]
            )
            hid_mx_of[c] = (hid_codes, hid_scales)

        def stage1_pair(c, first_plane):
            hid_codes, hid_scales = hid_mx_of[c]
            h1 = psum.tile([P, 2, width(c)], F32, tag="h1", bufs=3)
            for l in range(2):
                plane = first_plane + l
                nc.tensor.matmul_mx(
                    out=h1[:, l, :],
                    lhsT=w2_codes[:, P * plane : P * (plane + 1)].bitcast(FP8X4),
                    lhsT_scale=w2_scales[:, P * plane : P * (plane + 1)],
                    rhs=hid_codes[:].bitcast(FP8X4),
                    rhs_scale=hid_scales[:],
                    start=True,
                    stop=True,
                )
            return h1

        def relu(c, a, t, h):
            bias = (b2_lo, b2_hi)[a][:, t : t + 1]
            nc.scalar.activation(out=r_of[c, a][:, t, :], in_=h, func=ACT.Relu, bias=bias, scale=1.0)

        def stage1(c, a):
            r = work.tile([P, PACK, width(c)], F32, bufs=4)
            r_of[c, a] = r
            for pair in range(2):
                h1 = stage1_pair(c, PACK * a + 2 * pair)
                for l in range(2):
                    if (a, pair, l) == (0, 1, 1):
                        plane3_of[c] = h1[:, 1, :]
                        continue
                    relu(c, a, 2 * pair + l, h1[:, l, :])

        def plane3(c):
            rows_i = ROWS_TILE * CHUNK_TILES[c]
            nc.vector.scalar_tensor_tensor(
                out=r_of[c, 0][:, 3, :].rearrange("p (i j) -> p i j", j=NODES),
                in0=plane3_of[c].rearrange("p (i j) -> p i j", j=NODES),
                scalar=neg_b3[:],
                in1=b3_plus_x[:].unsqueeze(1).to_broadcast([P, rows_i, NODES]),
                op0=ALU.max,
                op1=ALU.add,
            )

        def new_s(c):
            s_grp = work.tile([P, 2, width(c), PACK], BF16, align_bytes=64, bufs=1)
            s_grp_of[c] = s_grp

        def add_nodes(c):
            first_i = ROWS_TILE * FIRST_TILE[c]
            for i in range(ROWS_TILE * CHUNK_TILES[c]):
                edges = slice(NODES * i, NODES * (i + 1))
                nc.gpsimd.tensor_tensor(
                    out=s_grp_of[c][:, 0, edges, :].rearrange("p (n k) t -> p n t k", k=PAIR),
                    in0=r_of[c, 0][:, :, edges].rearrange("p t (n k) -> p n t k", k=PAIR),
                    in1=x_words[:, first_i + i, :]
                    .unsqueeze(1)
                    .unsqueeze(3)
                    .to_broadcast([P, NODES // PAIR, PACK, PAIR]),
                    op=ALU.add,
                )

        def add_in_runs(s, r, z):
            nc.vector.tensor_tensor(
                out=s.rearrange("p (n i) t -> p n t i", i=RUN),
                in0=r[:].rearrange("p t (n i) -> p n t i", i=RUN),
                in1=z,
                op=ALU.add,
            )

        def add_z(c):
            z = z_words_of[c][:].bitcast(BF16).rearrange("p (n i) t -> p n t i", i=RUN)
            add_in_runs(s_grp_of[c][:, 1, :, :], r_of[c, 1], z)

        def quantise_s(c):
            s_codes = work.tile([P, 2, width(c)], U32, align_bytes=64)
            s_scales = work.tile([P, 2, width(c)], U8, align_bytes=64)
            nc.vector.quantize_mx(
                out=s_codes[:].rearrange("p a e -> p (a e)").bitcast(FP8X4),
                scales=s_scales[:].rearrange("p a e -> p (a e)"),
                in_=s_grp_of[c][:].rearrange("p a e t -> p (a e t)"),
            )
            s_mx_of[c] = (s_codes, s_scales)

        def stage2(c):
            s_codes, s_scales = s_mx_of[c]
            z2 = psum.tile([P, CHUNK_TILES[c], EDGE_F], F32, tag="z2")
            for n in range(CHUNK_TILES[c]):
                for a in range(2):
                    nc.tensor.matmul_mx(
                        out=z2[:, n, :],
                        lhsT=s_codes[:, a, P * n : P * (n + 1)].bitcast(FP8X4),
                        lhsT_scale=s_scales[:, a, P * n : P * (n + 1)],
                        rhs=wo_codes[:, EDGE_F * a : EDGE_F * (a + 1)].bitcast(FP8X4),
                        rhs_scale=wo_scales[:, EDGE_F * a : EDGE_F * (a + 1)],
                        start=(a == 0),
                        stop=(a == 1),
                    )
            ln_of[c]["z2"] = z2

        def add_bo(c):
            zb = work.tile([P, CHUNK_TILES[c], EDGE_F], F32, bufs=4)
            row_sum = work.tile([P, CHUNK_TILES[c]], F32, bufs=4)
            for n in range(CHUNK_TILES[c]):
                nc.vector.scalar_tensor_tensor(
                    out=zb[:, n, :],
                    in0=ln_of[c]["z2"][:, n, :],
                    scalar=1.0,
                    in1=bo_bc[:],
                    op0=ALU.mult,
                    op1=ALU.add,
                    accum_out=row_sum[:, n : n + 1],
                )
            ln_of[c]["zb"] = zb
            ln_of[c]["row_sum"] = row_sum

        def statistics(c):
            zb = ln_of[c]["zb"]
            neg_mean = work.tile([P, CHUNK_TILES[c]], F32, bufs=4)
            nc.scalar.mul(neg_mean[:], ln_of[c]["row_sum"][:], -1.0 / EDGE_F)
            squares = work.tile([P, CHUNK_TILES[c], EDGE_F], BF16)
            sq_sum = work.tile([P, CHUNK_TILES[c]], F32)
            rstd = work.tile([P, CHUNK_TILES[c]], F32, bufs=3)
            for n in range(CHUNK_TILES[c]):
                nc.scalar.activation(
                    out=squares[:, n, :],
                    in_=zb[:, n, :],
                    func=ACT.Square,
                    bias=neg_mean[:, n : n + 1],
                    scale=1.0,
                    accum_out=sq_sum[:, n : n + 1],
                )
            nc.scalar.activation(
                out=rstd[:], in_=sq_sum[:], func=ACT.Abs_reciprocal_sqrt, bias=eps_col[:], scale=1.0 / EDGE_F
            )
            ln_of[c]["rstd"] = rstd
            ln_of[c]["neg_mean"] = neg_mean

        def residual(c, tag="q", bufs=1):
            q = psum.tile([P, CHUNK_TILES[c], EDGE_F], F32, tag=tag, bufs=bufs)
            for n in range(CHUNK_TILES[c]):
                nc.tensor.matmul(
                    q[:, n, :].rearrange("p (g f) -> p g f", g=2),
                    lhsT=ident_bf[:],
                    rhs=z_cols[:, FIRST_TILE[c] + n, :, 1, :],
                    start=True,
                    stop=False,
                )
                nc.tensor.matmul(
                    q[:, n, :],
                    lhsT=ones_bf[:],
                    rhs=vec_rows[:, 2 * EDGE_F : 3 * EDGE_F],
                    start=False,
                    stop=True,
                )
            ln_of[c]["q"] = q

        def centre_and_gain(c):
            scaled = work.tile([P, CHUNK_TILES[c], EDGE_F], F32)
            for n in range(CHUNK_TILES[c]):
                nc.vector.scalar_tensor_tensor(
                    out=scaled[:, n, :],
                    in0=ln_of[c]["zb"][:, n, :],
                    scalar=ln_of[c]["neg_mean"][:, n : n + 1],
                    in1=g_ps[:],
                    op0=ALU.add,
                    op1=ALU.mult,
                )
            ln_of[c]["scaled"] = scaled

        def finish(c):
            result = work.tile([P, CHUNK_TILES[c], EDGE_F], F32, bufs=3)
            for n in range(CHUNK_TILES[c]):
                nc.vector.scalar_tensor_tensor(
                    out=result[:, n, :],
                    in0=ln_of[c]["scaled"][:, n, :],
                    scalar=ln_of[c]["rstd"][:, n : n + 1],
                    in1=ln_of[c]["q"][:, n, :],
                    op0=ALU.mult,
                    op1=ALU.add,
                )
            nc.sync.dma_start(
                out=out_rows[P * FIRST_TILE[c] : P * FIRST_TILE[c] + width(c), :].rearrange(
                    "(T p) f -> p T f", p=P
                ),
                in_=result[:],
            )

        bring_hid(0)
        nc.vector.tensor_copy(
            out=w2_grp[:, 0:512, :].rearrange("p (n i) t -> p n t i", i=RUN),
            in_=w2_raw[:, :, 0:512].rearrange("p t (n i) -> p n t i", i=RUN),
        )
        group_w2_hi(nc.vector.tensor_copy, 0)
        quantise_w2(0)
        quantise_hid(0)
        for plane_t in (2, 3):
            group_w2_hi(nc.scalar.copy, plane_t)
        group_w2_hi(nc.vector.tensor_copy, 1)
        node_tables()
        stage1(0, 0)
        plane3(0)
        new_s(0)
        quantise_w2(1)
        fill_node_j(0, 5)
        add_nodes(0)
        broadcast_bo_g()
        bring_hid(1)
        stage1(0, 1)
        bring_z(0)
        quantise_hid(1)
        group_wo()
        stage1(1, 0)
        bring_hid(2)
        add_z(0)
        plane3(1)
        quantise_wo()

        last = N_CHUNKS - 1
        for j in range(1, last):
            quantise_s(j - 1)
            quantise_hid(j + 1)
            new_s(j)
            add_nodes(j)
            stage1(j, 1)
            if j >= 3:
                residual(j - 3)
            if j >= 2:
                statistics(j - 2)
            bring_z(j)
            if j + 2 <= last:
                bring_hid(j + 2)
            stage1(j + 1, 0)
            stage2(j - 1)
            if j >= 3:
                finish(j - 3)
            add_z(j)
            if j >= 2:
                centre_and_gain(j - 2)
            add_bo(j - 1)
            plane3(j + 1)
            if j in (1, 2):
                fill_node_j(8 * j - 3, 8 * j + 5)

        quantise_s(last - 1)
        stage1(last, 1)
        residual(last - 3)
        statistics(last - 2)
        bring_z(last)
        stage2(last - 1)
        new_s(last)
        finish(last - 3)
        add_nodes(last)
        add_z(last)
        centre_and_gain(last - 2)
        quantise_s(last)
        residual(last - 2)
        residual(last - 1, tag="hid_t")
        residual(last, tag="h1", bufs=3)
        add_bo(last - 1)
        stage2(last)
        statistics(last - 1)
        finish(last - 2)
        add_bo(last)
        statistics(last)
        centre_and_gain(last - 1)
        finish(last - 1)
        centre_and_gain(last)
        finish(last)
